import numpy as np
import ml_dtypes


def mxq(x, axis, fmt="e4m3"):
    dtype, down = {"e4m3": (ml_dtypes.float8_e4m3fn, 7), "e5m2": (ml_dtypes.float8_e5m2, 14)}[fmt]
    v = np.moveaxis(np.asarray(x, np.float32).astype(ml_dtypes.bfloat16).astype(np.float64), axis, -1)
    blocks = v.reshape(v.shape[:-1] + (-1, 32))
    amax = np.abs(blocks).max(-1, keepdims=True)
    byte = np.maximum(np.where(amax > 0, np.frexp(amax)[1] - 1 + 127, 0) - down, 1)
    scale = np.exp2(byte - 127.0)
    codes = (blocks / scale).astype(np.float32).astype(dtype).astype(np.float64)
    return np.moveaxis((codes * scale).reshape(v.shape), -1, axis)


WIDE = False


def mx_kscale(k):
    if not WIDE:
        return np.ones(k)
    levels = np.array([10, -10, 5, -5, 0])
    a = np.random.permutation(np.resize(levels, k // 512 * 4)).reshape(k // 512, 4)
    idx = np.arange(k)
    return np.exp2(a[idx // 512, idx % 128 // 32])


BF16 = ml_dtypes.bfloat16


def bf(x):
    return np.asarray(x, np.float32).astype(BF16)


def f64(x):
    return np.asarray(x).astype(np.float64)


E2M1 = np.array([0.0, 0.5, 1.0, 1.5, 2.0, 3.0, 4.0, 6.0, -0.0, -0.5, -1.0, -1.5, -2.0, -3.0, -4.0, -6.0])


def pack_weight(w, fmt):
    k, n = w.shape
    w = f64(bf(w)).reshape(k // 32, 32, n)
    amax = np.abs(w).max(1)
    if fmt == "e4m3":
        byte = np.frexp(amax)[1] - 1 + 127 - 7
    else:
        mant, ex = np.frexp(amax / 6.0)
        byte = np.where(mant > 0.5, ex, ex - 1) + 127
    byte = np.clip(np.where(amax > 0, byte, 1), 1, 254)
    scaled = (w * np.exp2(127.0 - byte)[:, None, :]).reshape(k, n).astype(np.float32)
    by_word = np.ascontiguousarray(scaled.reshape(k // 512, 128, 4, n).transpose(0, 1, 3, 2))
    if fmt == "e4m3":
        words = by_word.astype(ml_dtypes.float8_e4m3fn).view(np.uint8)
    else:
        c = by_word.astype(ml_dtypes.float4_e2m1fn).view(np.uint8) & 0xF
        words = c[..., 0::2] | (c[..., 1::2] << 4)
    return np.ascontiguousarray(words), np.ascontiguousarray(byte.astype(np.uint8).reshape(k // 512, 16, n))


def unpack_weight(words, scales, fmt):
    g, p, n, _ = words.shape
    if fmt == "e4m3":
        vals = np.ascontiguousarray(words).view(ml_dtypes.float8_e4m3fn).astype(np.float64)
    else:
        nib = np.empty((g, p, n, 4), np.uint8)
        nib[..., 0::2] = words & 0xF
        nib[..., 1::2] = words >> 4
        vals = E2M1[nib]
    vals = vals * np.repeat(np.exp2(scales.astype(np.float64) - 127.0), 8, axis=1)[..., None]
    return vals.transpose(0, 1, 3, 2).reshape(g * 512, n)


B, N, C, H, D = 8, 1024, 1024, 4, 32
EPS = 1e-12
SCALE = float(D) ** 0.25
VG = 4.0
FMT = "e4m3"


def normalize(t):
    n = np.sqrt((t * t).sum(-1, keepdims=True))
    return t / np.maximum(n, EPS)


def heads(t):
    return t.reshape(B, N, H, D).transpose(0, 2, 1, 3)


def setup_inputs():
    s = mx_kscale(C)
    x = bf(np.random.standard_normal((B, N, C)) * s)
    Wk = np.random.standard_normal((H * D, C)) / np.sqrt(C) / s
    Wk_words, Wk_scales = pack_weight(np.ascontiguousarray(Wk.T), FMT)
    bk = bf(np.random.standard_normal(H * D) * 0.1)
    Wv = np.random.standard_normal((H * D, C)) * VG / np.sqrt(C) / s
    Wv_words, Wv_scales = pack_weight(np.ascontiguousarray(Wv.T), FMT)
    bv = bf(np.random.standard_normal(H * D) * 0.1)
    return {'x': x,
            'Wk_words': Wk_words,
            'Wk_scales': Wk_scales,
            'bk': bk,
            'Wv_words': Wv_words,
            'Wv_scales': Wv_scales,
            'bv': bv}


def reference(x, Wk_words, Wk_scales, bk, Wv_words, Wv_scales, bv):
    xq = mxq(f64(x), 2, 'e4m3')
    k = heads((xq @ unpack_weight(Wk_words, Wk_scales, FMT)) + f64(bk))
    v = heads((xq @ unpack_weight(Wv_words, Wv_scales, FMT)) + f64(bv))
    kn = normalize(k) * SCALE
    vN = v / N
    kk = (kn[..., :, None] * kn[..., None, :]).reshape(B, H, N, D * D)
    vq = mxq(vN, 2, 'e4m3')
    mod_v = mxq(kk, 2, 'e4m3').transpose(0, 1, 3, 2) @ vq
    mod_n = kk.sum(2) / N
    kv_mod = np.concatenate([mod_n[..., None], mod_v], axis=-1).reshape(B, H, D, D, D + 1)
    kv_v = mxq(kn, 2, 'e4m3').transpose(0, 1, 3, 2) @ vq
    kv_n = kn.sum(2) / N
    kv = np.concatenate([kv_n[..., None], kv_v], axis=-1)
    vsum = np.concatenate([np.ones((B, H, 1)), vN.sum(2)], axis=-1)[:, :, None, :]
    return kv_mod, kv, vsum

@@ -1,0 +1,438 @@
+from contextlib import ExitStack
+
+import concourse.mybir as mybir
+from concourse.masks import make_identity
+
+F32 = mybir.dt.float32
+BF16 = mybir.dt.bfloat16
+U8 = mybir.dt.uint8
+U32 = mybir.dt.uint32
+I32 = mybir.dt.int32
+FP8X4 = mybir.dt.float8_e4m3fn_x4
+ACT = mybir.ActivationFunctionType
+ALU = mybir.AluOpType
+AX = mybir.AxisListType
+
+P = 128
+PACK = 4
+K_PASS = P * PACK
+B, N_TOK, C, H, D = 8, 1024, 1024, 4, 32
+GROUPS = N_TOK // K_PASS
+C_PASSES = C // K_PASS
+EPS = 1e-12
+SCALE_SQ = 32.0**0.5
+BLK = 8
+N_BLK = D // BLK
+MAIN = 512
+TAIL = 128
+PAIRS = MAIN + TAIL
+ROW_START = {0: 0, 1: 256, 3: 448, 2: 512}
+GPSIMD_ROWS = (1, 3)
+
+FLOPS = 2 * B * N_TOK * C * 2 * H * D + 2 * B * H * N_TOK * D * D * D + 2 * B * H * N_TOK * D * D
+
+
+def tile_taylorsoftmaxattention_pa_t_kernel(
+    tc, x, Wk_words, Wk_scales, bk, Wv_words, Wv_scales, bv, out_0, out_1, out_2
+):
+    nc = tc.nc
+    with ExitStack() as ctx:
+        const = ctx.enter_context(tc.tile_pool(name="const", bufs=1))
+        x_pool = ctx.enter_context(tc.tile_pool(name="x_pool", bufs=3))
+        work = ctx.enter_context(tc.tile_pool(name="work", bufs=2))
+        words = ctx.enter_context(tc.tile_pool(name="words", bufs=3))
+        small_words = ctx.enter_context(tc.tile_pool(name="small_words", bufs=4))
+        turn_ps = ctx.enter_context(tc.psum_pool(name="turn_ps", bufs=2))
+        proj_ps = ctx.enter_context(tc.psum_pool(name="proj_ps", bufs=2))
+        ktok_ps = ctx.enter_context(tc.psum_pool(name="ktok_ps", bufs=2))
+        main_ps = ctx.enter_context(tc.psum_pool(name="main_ps", bufs=1))
+        misc_ps = ctx.enter_context(tc.psum_pool(name="misc_ps", bufs=1))
+        ctx.enter_context(tc.manual_schedule())
+
+        ident = const.tile([P, P], F32)
+        make_identity(nc, ident[:])
+
+        w_words = const.tile([P, 2 * C_PASSES, P], U32, align_bytes=64)
+        w_scales = const.tile([P, 2 * C_PASSES, P], U8, align_bytes=64)
+        nc.vector.memset(w_scales[:].bitcast(I32), 0)
+        for w, (codes, scales) in enumerate(((Wk_words, Wk_scales), (Wv_words, Wv_scales))):
+            for c in range(C_PASSES):
+                nc.sync.dma_start(
+                    out=w_words[:, C_PASSES * w + c, :].bitcast(I32),
+                    in_=codes[c].rearrange("p n t -> p (n t)").bitcast(I32),
+                )
+            for quad in range(4):
+                nc.sync.dma_start(
+                    out=w_scales[32 * quad : 32 * quad + 4, C_PASSES * w : C_PASSES * (w + 1), :].bitcast(I32),
+                    in_=scales[:, 4 * quad : 4 * quad + 4, :].rearrange("c r n -> r c n").bitcast(I32),
+                )
+
+        bias_rows = const.tile([P, P], BF16)
+        nc.vector.memset(bias_rows[:], 0.0)
+        nc.sync.dma_start(out=bias_rows[0:1, :], in_=bk.unsqueeze(0))
+        nc.sync.dma_start(out=bias_rows[1:2, :], in_=bv.unsqueeze(0))
+        bias_rows_f = const.tile([P, P], F32)
+        nc.vector.tensor_copy(out=bias_rows_f[:], in_=bias_rows[:])
+        bias_ps = turn_ps.tile([P, P], F32, tag="turn")
+        nc.tensor.transpose(bias_ps[:], bias_rows_f[:], ident[:])
+        bias_col = const.tile([P, 2], F32)
+        nc.scalar.copy(out=bias_col[:, 0:1], in_=bias_ps[:, 0:1])
+        nc.scalar.mul(out=bias_col[:, 1:2], in_=bias_ps[:, 1:2], mul=1.0 / N_TOK)
+
+        rep_one = const.tile([P, D], F32)
+        nc.vector.tensor_reduce(
+            out=rep_one[:], in_=ident[:].rearrange("k (h i) -> k i h", h=H), axis=AX.X, op=ALU.add
+        )
+        rep = const.tile([P, N_BLK, D], F32)
+        nc.vector.tensor_copy(out=rep[:], in_=rep_one[:].unsqueeze(1).to_broadcast([P, N_BLK, D]))
+        rep_head = const.tile([P, H, P], F32)
+        nc.vector.memset(rep_head[:], 0.0)
+        for h in range(H):
+            own = slice(D * h, D * (h + 1))
+            nc.vector.tensor_copy(out=rep_head[own, h, :], in_=rep[own].rearrange("k J i -> k (J i)"))
+        ones = const.tile([P, PACK], F32)
+        nc.vector.memset(ones[:], 1.0)
+
+        v_diag = [const.tile([P, H, 640], BF16, name="v_diag%d" % n, align_bytes=64) for n in range(2)]
+        kn_tok = [const.tile([P, PACK, P + 4], F32, name="kn_tok%d" % n) for n in range(4)]
+        for n in range(2):
+            nc.vector.memset(v_diag[n][:], 0.0)
+        for n in range(4):
+            nc.scalar.copy(out=kn_tok[n][:, :, P : P + 1], in_=ones[:].unsqueeze(2))
+        v_sums = const.tile([P, B * GROUPS], F32)
+
+        n_groups = B * GROUPS
+        held = {}
+
+        def load(g):
+            b, part = divmod(g, GROUPS)
+            xs = x_pool.tile([P, PACK, C], BF16, tag="xs")
+            nc.sync.dma_start(
+                out=xs[:],
+                in_=x[b, K_PASS * part : K_PASS * (part + 1), :].rearrange("(p t) c -> p t c", t=PACK),
+            )
+            held["xs", g] = xs
+
+        def turn_x(g):
+            xs = held["xs", g]
+            x_grouped = work.tile([P, C_PASSES * K_PASS * PACK], BF16, tag="x_grouped", align_bytes=64)
+            grouped_words = x_grouped[:].bitcast(F32).rearrange("p (c n u) -> p c n u", c=C_PASSES, u=2)
+            for c in range(C_PASSES):
+                for half in range(2):
+                    turned = turn_ps.tile([P, 2, 2 * P], F32, tag="turn")
+                    for u in range(2):
+                        for tl in range(2):
+                            x_words = xs[:, 2 * half + tl, :].bitcast(F32)
+                            nc.tensor.transpose(
+                                turned[:, u, P * tl : P * (tl + 1)],
+                                x_words[:, 256 * c + u : 256 * (c + 1) : 2],
+                                ident[:],
+                            )
+                    nc.scalar.copy(
+                        out=grouped_words[:, c, 2 * P * half : 2 * P * (half + 1), :],
+                        in_=turned[:].rearrange("p u n -> p n u"),
+                    )
+            held["x_grouped", g] = x_grouped
+
+        def quantise_x(g):
+            x_q = work.tile([P, C_PASSES * K_PASS], U32, tag="x_q", align_bytes=64)
+            x_s = work.tile([P, C_PASSES * K_PASS], U8, tag="x_s", align_bytes=64)
+            nc.vector.quantize_mx(out=x_q[:].bitcast(FP8X4), scales=x_s[:], in_=held["x_grouped", g][:])
+            held["x_q", g] = (x_q, x_s)
+
+        def project(g):
+            x_q, x_s = held["x_q", g]
+            sums = []
+            for w in range(2):
+                acc = proj_ps.tile([P, K_PASS], F32, tag="proj")
+                for c in range(C_PASSES):
+                    cols = slice(K_PASS * c, K_PASS * (c + 1))
+                    nc.tensor.matmul_mx(
+                        out=acc[:],
+                        lhsT=w_words[:, C_PASSES * w + c, :].bitcast(FP8X4),
+                        lhsT_scale=w_scales[:, C_PASSES * w + c, :],
+                        rhs=x_q[:, cols].bitcast(FP8X4),
+                        rhs_scale=x_s[:, cols],
+                        start=(c == 0),
+                        stop=(c == C_PASSES - 1),
+                    )
+                sums.append(acc)
+            kT = work.tile([P, K_PASS], F32, tag="kT")
+            vT = work.tile([P, K_PASS], F32, tag="vT")
+            nc.scalar.activation(out=kT[:], in_=sums[0][:], func=ACT.Identity, bias=bias_col[:, 0:1], scale=1.0)
+            nc.scalar.activation(
+                out=vT[:],
+                in_=sums[1][:],
+                func=ACT.Identity,
+                bias=bias_col[:, 1:2],
+                scale=1.0 / N_TOK,
+                accum_out=v_sums[:, g : g + 1],
+            )
+            held["kT", g] = kT
+            held["vT", g] = vT
+
+        def to_tokens(g):
+            k_tok = ktok_ps.tile([P, PACK, P], F32, tag="k_tok")
+            v_tok = turn_ps.tile([P, PACK, P], F32, tag="turn")
+            for t in range(PACK):
+                nc.tensor.transpose(k_tok[:, t, :], held["kT", g][:, P * t : P * (t + 1)], ident[:])
+            for t in range(PACK):
+                nc.tensor.transpose(v_tok[:, t, :], held["vT", g][:, P * t : P * (t + 1)], ident[:])
+            squares = work.tile([P, PACK * H, D], F32, tag="squares")
+            nc.scalar.activation(
+                out=squares[:], in_=k_tok[:].rearrange("p t (h d) -> p (t h) d", d=D), func=ACT.Square
+            )
+            nc.scalar.copy(
+                out=v_diag[g % 2][:, :, 0 : D * PACK].rearrange("p h (e t) -> p h e t", t=PACK),
+                in_=v_tok[:].rearrange("p t (h e) -> p h e t", h=H),
+            )
+            held["k_tok", g] = k_tok
+            held["squares", g] = squares
+
+        def scale_k(g, factor, tag):
+            scaled = work.tile([P, P, PACK], F32, tag=tag, name=tag)
+            nc.vector.tensor_tensor(
+                out=scaled[:].rearrange("p (h d) t -> p h d t", h=H),
+                in0=held["k_tok", g][:].rearrange("p t (h d) -> p h d t", h=H),
+                in1=factor[:].rearrange("p (t h) -> p h t", h=H).unsqueeze(2).to_broadcast([P, H, D, PACK]),
+                op=ALU.mult,
+            )
+            return scaled
+
+        def norm(g):
+            sumsq = work.tile([P, PACK * H], F32, tag="sumsq")
+            nc.vector.tensor_reduce(out=sumsq[:], in_=held["squares", g][:], axis=AX.X, op=ALU.add)
+            floored = work.tile([P, PACK * H], F32, tag="floored")
+            nc.vector.tensor_scalar(
+                out=floored[:], in0=sumsq[:], scalar1=EPS * EPS, scalar2=1.0 / SCALE_SQ, op0=ALU.max, op1=ALU.mult
+            )
+            r2 = work.tile([P, PACK * H], F32, tag="r2")
+            nc.vector.reciprocal(out=r2[:], in_=floored[:])
+            r1 = work.tile([P, PACK * H], F32, tag="r1")
+            nc.scalar.activation(out=r1[:], in_=r2[:], func=ACT.Sqrt)
+            held["k_r2", g] = scale_k(g, r2, "k_r2")
+            v_q = small_words.tile([P, H * P], U32, tag="v_q", align_bytes=64)
+            v_s = small_words.tile([P, H * P], U8, tag="v_s", align_bytes=64)
+            nc.vector.quantize_mx(
+                out=v_q[:].bitcast(FP8X4),
+                scales=v_s[:],
+                in_=v_diag[g % 2][:].rearrange("p h x -> p (h x)")[:, 0 : H * P * PACK],
+            )
+            held["v_q", g] = (v_q, v_s)
+            kn = scale_k(g, r1, "kn")
+            held["kn", g] = kn
+            nc.scalar.copy(out=kn_tok[g % 4][:, :, 0:P], in_=kn[:].rearrange("p f t -> p t f"))
+            kn_bf = work.tile([P, P * PACK], BF16, tag="kn_bf", align_bytes=64)
+            nc.scalar.copy(out=kn_bf[:], in_=kn[:].rearrange("p f t -> p (f t)"))
+            held["kn_bf", g] = kn_bf
+
+        def quantise_kn(g):
+            kn_q = small_words.tile([P, P], U32, tag="kn_q", align_bytes=64)
+            kn_s = small_words.tile([P, P], U8, tag="kn_s", align_bytes=64)
+            nc.vector.quantize_mx(out=kn_q[:].bitcast(FP8X4), scales=kn_s[:], in_=held["kn_bf", g][:])
+            held["kn_q", g] = (kn_q, kn_s)
+
+        def products(g):
+            k_tok, k_r2, kn = held["k_tok", g], held["k_r2", g], held["kn", g]
+            kk_bf = work.tile([P, H, PAIRS, PACK], BF16, tag="kk_bf", align_bytes=64)
+            for h in range(H):
+                for row in range(N_BLK):
+                    width = D - BLK * row
+                    first = D * h + BLK * row
+                    shape = [P, BLK, width, PACK]
+                    out = kk_bf[:, h, ROW_START[row] : ROW_START[row] + BLK * width, :].rearrange(
+                        "p (i j) t -> p i j t", i=BLK
+                    )
+                    if row in GPSIMD_ROWS:
+                        nc.gpsimd.tensor_tensor(
+                            out=out,
+                            in0=kn[:, first : first + BLK, :].unsqueeze(2).to_broadcast(shape),
+                            in1=kn[:, first : first + width, :].unsqueeze(1).to_broadcast(shape),
+                            op=ALU.mult,
+                        )
+                    else:
+                        nc.vector.tensor_tensor(
+                            out=out,
+                            in0=k_tok[:, :, first : first + BLK]
+                            .rearrange("p t i -> p i t")
+                            .unsqueeze(2)
+                            .to_broadcast(shape),
+                            in1=k_r2[:, first : first + width, :].unsqueeze(1).to_broadcast(shape),
+                            op=ALU.mult,
+                        )
+            held["kk_bf", g] = kk_bf
+
+        def quantise_products(g):
+            kk_bf = held["kk_bf", g]
+            kk_q = words.tile([P, H, PAIRS], U32, tag="kk_q", align_bytes=64)
+            kk_s = words.tile([P, H, PAIRS], U8, tag="kk_s", align_bytes=64)
+            for h in range(H):
+                for cols in (slice(0, MAIN), slice(MAIN, PAIRS)):
+                    nc.vector.quantize_mx(
+                        out=kk_q[:, h, cols].bitcast(FP8X4),
+                        scales=kk_s[:, h, cols],
+                        in_=kk_bf[:, h, cols, :].rearrange("p c t -> p (c t)"),
+                    )
+            held["kk_q", g] = (kk_q, kk_s)
+
+        def moment_passes(out, g, cols):
+            v_q, v_s = held["v_q", g]
+            kk_q, kk_s = held["kk_q", g]
+            for h in range(H):
+                nc.tensor.matmul_mx(
+                    out=out,
+                    lhsT=v_q[:, P * h : P * (h + 1)].bitcast(FP8X4),
+                    lhsT_scale=v_s[:, P * h : P * (h + 1)],
+                    rhs=kk_q[:, h, cols].bitcast(FP8X4),
+                    rhs_scale=kk_s[:, h, cols],
+                    start=(g % GROUPS == 0 and h == 0),
+                    stop=(g % GROUPS == GROUPS - 1 and h == H - 1),
+                )
+
+        def main_passes(g):
+            if g % GROUPS == 0:
+                z_main = main_ps.tile([P, MAIN], F32, tag="z_main")
+                held["z_main", g // GROUPS] = z_main
+            moment_passes(held["z_main", g // GROUPS][:], g, slice(0, MAIN))
+
+        def float_sums(b):
+            o_tile = work.tile([P, H, BLK, D + 1], F32, tag="o_tile")
+            kv_tile = work.tile([P, D + 1], F32, tag="kv_tile")
+            held["o_tile", b] = o_tile
+            held["kv_tile", b] = kv_tile
+            mn = misc_ps.tile([P, P + 1], F32, tag="misc")
+            for part in range(GROUPS):
+                tok = kn_tok[(GROUPS * b + part) % 4]
+                for t in range(PACK):
+                    nc.tensor.matmul(
+                        out=mn[:],
+                        lhsT=tok[:, t, 0:P],
+                        rhs=tok[:, t, 0 : P + 1],
+                        start=(part == 0 and t == 0),
+                        stop=(part == GROUPS - 1 and t == PACK - 1),
+                    )
+            mn_sb = work.tile([P, P + 1], F32, tag="mn_sb")
+            nc.scalar.mul(out=mn_sb[:], in_=mn[:], mul=1.0 / N_TOK)
+            nc.scalar.copy(out=kv_tile[:, 0:1], in_=mn_sb[:, P : P + 1])
+            q = misc_ps.tile([P, P], F32, tag="misc")
+            for h in range(H):
+                own = slice(D * h, D * (h + 1))
+                nc.tensor.matmul(out=q[:, own], lhsT=rep_head[:, h, :], rhs=mn_sb[:, own], start=True, stop=True)
+            for J in range(N_BLK):
+                rows = slice(D * J, D * (J + 1))
+                nc.scalar.copy(
+                    out=o_tile[rows, :, :, 0:1],
+                    in_=q[rows, :].rearrange("p (h j) -> p h j", h=H)[:, :, BLK * J : BLK * (J + 1)].unsqueeze(3),
+                )
+
+        def spread(z_sq, bank, row):
+            width = D - BLK * row
+            start = ROW_START[row] % MAIN
+            block_row = bank[:, start : start + BLK * width]
+            nc.scalar.copy(
+                out=z_sq[:, :, row:N_BLK, BLK * row : BLK * (row + 1)],
+                in_=block_row.rearrange("p (a J l) -> p l J a", a=BLK, l=BLK),
+            )
+            if width > BLK:
+                nc.scalar.copy(
+                    out=z_sq[:, :, row, BLK * (row + 1) : D],
+                    in_=block_row.rearrange("p (a j) -> p a j", a=BLK)[:, :, BLK:width],
+                )
+
+        def square_up(b):
+            z_tail = misc_ps.tile([P, TAIL], F32, tag="misc")
+            for part in range(GROUPS):
+                moment_passes(z_tail[:], GROUPS * b + part, slice(MAIN, PAIRS))
+            z_sq = work.tile([P, BLK, N_BLK, D], F32, tag="z_sq")
+            for row in range(N_BLK):
+                spread(z_sq, held["z_main", b] if ROW_START[row] < MAIN else z_tail, row)
+            held["z_sq", b] = z_sq
+
+        def outputs(b):
+            o_tile, kv_tile, z_sq = held["o_tile", b], held["kv_tile", b], held["z_sq", b]
+            kv_ps = misc_ps.tile([P, P], F32, tag="misc")
+            for part in range(GROUPS):
+                v_q, v_s = held["v_q", GROUPS * b + part]
+                kn_q, kn_s = held["kn_q", GROUPS * b + part]
+                for h in range(H):
+                    nc.tensor.matmul_mx(
+                        out=kv_ps[:],
+                        lhsT=kn_q[:].bitcast(FP8X4),
+                        lhsT_scale=kn_s[:],
+                        rhs=v_q[:, P * h : P * (h + 1)].bitcast(FP8X4),
+                        rhs_scale=v_s[:, P * h : P * (h + 1)],
+                        start=(part == 0 and h == 0),
+                        stop=(part == GROUPS - 1 and h == H - 1),
+                    )
+            for h in range(H):
+                own = slice(D * h, D * (h + 1))
+                nc.scalar.copy(out=kv_tile[own, 1 : D + 1], in_=kv_ps[own, own])
+            nc.scalar.dma_start(out=out_1[b].rearrange("h d c -> (h d) c"), in_=kv_tile[:])
+            for half in range(2):
+                turned = turn_ps.tile([P, PACK, P], F32, tag="turn")
+                for n in range(PACK):
+                    nc.tensor.transpose(
+                        turned[:, n, :], z_sq[:, PACK * half + n, :, :].rearrange("p J i -> p (J i)"), ident[:]
+                    )
+                nc.scalar.copy(
+                    out=o_tile[:, :, PACK * half : PACK * (half + 1), 1 : D + 1],
+                    in_=turned[:].rearrange("p l (h e) -> p h l e", h=H),
+                )
+            for J in range(N_BLK):
+                nc.scalar.dma_start(
+                    out=out_0[b, :, :, BLK * J : BLK * (J + 1), :].rearrange("h i l c -> i h (l c)"),
+                    in_=o_tile[D * J : D * (J + 1)].rearrange("p h l c -> p h (l c)"),
+                )
+
+        for g in range(3):
+            load(g)
+        for g in range(2):
+            turn_x(g)
+            quantise_x(g)
+            project(g)
+        to_tokens(0)
+        norm(0)
+        quantise_kn(0)
+        for g in range(n_groups):
+            if g + 1 < n_groups:
+                to_tokens(g + 1)
+            products(g)
+            if g >= 1:
+                main_passes(g - 1)
+            if g >= GROUPS and g % GROUPS == 0:
+                square_up(g // GROUPS - 1)
+            if g + 3 < n_groups:
+                load(g + 3)
+            if g + 2 < n_groups:
+                turn_x(g + 2)
+                quantise_x(g + 2)
+            if g + 1 < n_groups:
+                norm(g + 1)
+            quantise_products(g)
+            if g + 1 < n_groups:
+                quantise_kn(g + 1)
+            if g + 2 < n_groups:
+                project(g + 2)
+            if g >= GROUPS and g % GROUPS == 0:
+                outputs(g // GROUPS - 1)
+            if g % GROUPS == GROUPS - 1:
+                float_sums(g // GROUPS)
+        main_passes(n_groups - 1)
+        square_up(B - 1)
+        outputs(B - 1)
+
+        sums_sq = const.tile([P, P], F32)
+        nc.vector.memset(sums_sq[:], 0.0)
+        nc.vector.tensor_tensor(
+            out=sums_sq[:, 0:B], in0=v_sums[:, 0 : B * GROUPS : 2], in1=v_sums[:, 1 : B * GROUPS : 2], op=ALU.add
+        )
+        sums_ps = turn_ps.tile([P, P], F32, tag="turn")
+        nc.tensor.transpose(sums_ps[:], sums_sq[:], ident[:])
+        vsum_tile = const.tile([P, H, D + 1], F32)
+        nc.vector.memset(vsum_tile[0:D, :, 0:1], 1.0)
+        nc.vector.tensor_copy(
+            out=vsum_tile[0:D, :, 1 : D + 1], in_=sums_ps[0:D, :].rearrange("p (h e) -> p h e", h=H)
+        )
+        nc.scalar.dma_start(
+            out=out_2.rearrange("b h o c -> b (h o c)"), in_=vsum_tile[0:B].rearrange("p h c -> p (h c)")
+        )

@@ -41,13 +41,27 @@ def tile_taylorsoftmaxattention_pa_t_kernel(
         x_pool = ctx.enter_context(tc.tile_pool(name="x_pool", bufs=3))
         work = ctx.enter_context(tc.tile_pool(name="work", bufs=2))
         words = ctx.enter_context(tc.tile_pool(name="words", bufs=3))
-        small_words = ctx.enter_context(tc.tile_pool(name="small_words", bufs=4))
+        single = ctx.enter_context(tc.tile_pool(name="single", bufs=1))
         turn_ps = ctx.enter_context(tc.psum_pool(name="turn_ps", bufs=2))
         proj_ps = ctx.enter_context(tc.psum_pool(name="proj_ps", bufs=2))
         ktok_ps = ctx.enter_context(tc.psum_pool(name="ktok_ps", bufs=2))
         main_ps = ctx.enter_context(tc.psum_pool(name="main_ps", bufs=1))
         misc_ps = ctx.enter_context(tc.psum_pool(name="misc_ps", bufs=1))
         ctx.enter_context(tc.manual_schedule())
+
+        n_groups = B * GROUPS
+        held = {}
+
+        def load(g):
+            b, part = divmod(g, GROUPS)
+            xs = x_pool.tile([P, PACK, C], BF16, tag="xs")
+            nc.sync.dma_start(
+                out=xs[:],
+                in_=x[b, K_PASS * part : K_PASS * (part + 1), :].rearrange("(p t) c -> p t c", t=PACK),
+            )
+            held["xs", g] = xs
+
+        load(0)
 
         ident = const.tile([P, P], F32)
         make_identity(nc, ident[:])
@@ -71,14 +85,8 @@ def tile_taylorsoftmaxattention_pa_t_kernel(
         nc.vector.memset(bias_rows[:], 0.0)
         nc.sync.dma_start(out=bias_rows[0:1, :], in_=bk.unsqueeze(0))
         nc.sync.dma_start(out=bias_rows[1:2, :], in_=bv.unsqueeze(0))
-        bias_rows_f = const.tile([P, P], F32)
-        nc.vector.tensor_copy(out=bias_rows_f[:], in_=bias_rows[:])
-        bias_ps = turn_ps.tile([P, P], F32, tag="turn")
-        nc.tensor.transpose(bias_ps[:], bias_rows_f[:], ident[:])
-        bias_col = const.tile([P, 2], F32)
-        nc.scalar.copy(out=bias_col[:, 0:1], in_=bias_ps[:, 0:1])
-        nc.scalar.mul(out=bias_col[:, 1:2], in_=bias_ps[:, 1:2], mul=1.0 / N_TOK)
-
+        load(1)
+        load(2)
         rep_one = const.tile([P, D], F32)
         nc.vector.tensor_reduce(
             out=rep_one[:], in_=ident[:].rearrange("k (h i) -> k i h", h=H), axis=AX.X, op=ALU.add
@@ -100,18 +108,6 @@ def tile_taylorsoftmaxattention_pa_t_kernel(
         for n in range(4):
             nc.scalar.copy(out=kn_tok[n][:, :, P : P + 1], in_=ones[:].unsqueeze(2))
         v_sums = const.tile([P, B * GROUPS], F32)
-
-        n_groups = B * GROUPS
-        held = {}
-
-        def load(g):
-            b, part = divmod(g, GROUPS)
-            xs = x_pool.tile([P, PACK, C], BF16, tag="xs")
-            nc.sync.dma_start(
-                out=xs[:],
-                in_=x[b, K_PASS * part : K_PASS * (part + 1), :].rearrange("(p t) c -> p t c", t=PACK),
-            )
-            held["xs", g] = xs
 
         def turn_x(g):
             xs = held["xs", g]
@@ -211,14 +207,6 @@ def tile_taylorsoftmaxattention_pa_t_kernel(
             r1 = work.tile([P, PACK * H], F32, tag="r1")
             nc.scalar.activation(out=r1[:], in_=r2[:], func=ACT.Sqrt)
             held["k_r2", g] = scale_k(g, r2, "k_r2")
-            v_q = small_words.tile([P, H * P], U32, tag="v_q", align_bytes=64)
-            v_s = small_words.tile([P, H * P], U8, tag="v_s", align_bytes=64)
-            nc.vector.quantize_mx(
-                out=v_q[:].bitcast(FP8X4),
-                scales=v_s[:],
-                in_=v_diag[g % 2][:].rearrange("p h x -> p (h x)")[:, 0 : H * P * PACK],
-            )
-            held["v_q", g] = (v_q, v_s)
             kn = scale_k(g, r1, "kn")
             held["kn", g] = kn
             nc.scalar.copy(out=kn_tok[g % 4][:, :, 0:P], in_=kn[:].rearrange("p f t -> p t f"))
@@ -226,15 +214,25 @@ def tile_taylorsoftmaxattention_pa_t_kernel(
             nc.scalar.copy(out=kn_bf[:], in_=kn[:].rearrange("p f t -> p (f t)"))
             held["kn_bf", g] = kn_bf
 
+        def quantise_v(g):
+            v_q = words.tile([P, H * P], U32, tag="v_q", align_bytes=64)
+            v_s = words.tile([P, H * P], U8, tag="v_s", align_bytes=64)
+            nc.vector.quantize_mx(
+                out=v_q[:].bitcast(FP8X4),
+                scales=v_s[:],
+                in_=v_diag[g % 2][:].rearrange("p h x -> p (h x)")[:, 0 : H * P * PACK],
+            )
+            held["v_q", g] = (v_q, v_s)
+
         def quantise_kn(g):
-            kn_q = small_words.tile([P, P], U32, tag="kn_q", align_bytes=64)
-            kn_s = small_words.tile([P, P], U8, tag="kn_s", align_bytes=64)
+            kn_q = words.tile([P, P], U32, tag="kn_q", align_bytes=64)
+            kn_s = words.tile([P, P], U8, tag="kn_s", align_bytes=64)
             nc.vector.quantize_mx(out=kn_q[:].bitcast(FP8X4), scales=kn_s[:], in_=held["kn_bf", g][:])
             held["kn_q", g] = (kn_q, kn_s)
 
         def products(g):
             k_tok, k_r2, kn = held["k_tok", g], held["k_r2", g], held["kn", g]
-            kk_bf = work.tile([P, H, PAIRS, PACK], BF16, tag="kk_bf", align_bytes=64)
+            kk_bf = single.tile([P, H, PAIRS, PACK], BF16, tag="kk_bf", align_bytes=64)
             for h in range(H):
                 for row in range(N_BLK):
                     width = D - BLK * row
@@ -384,33 +382,40 @@ def tile_taylorsoftmaxattention_pa_t_kernel(
                     in_=o_tile[D * J : D * (J + 1)].rearrange("p h l c -> p h (l c)"),
                 )
 
-        for g in range(3):
-            load(g)
-        for g in range(2):
-            turn_x(g)
-            quantise_x(g)
-            project(g)
+        turn_x(0)
+        turn_x(1)
+        bias_rows_f = const.tile([P, P], F32)
+        nc.vector.tensor_copy(out=bias_rows_f[:], in_=bias_rows[:])
+        bias_ps = turn_ps.tile([P, P], F32, tag="turn")
+        nc.tensor.transpose(bias_ps[:], bias_rows_f[:], ident[:])
+        bias_col = const.tile([P, 2], F32)
+        nc.scalar.copy(out=bias_col[:, 0:1], in_=bias_ps[:, 0:1])
+        nc.scalar.mul(out=bias_col[:, 1:2], in_=bias_ps[:, 1:2], mul=1.0 / N_TOK)
+        quantise_x(0)
+        quantise_x(1)
+        project(0)
         to_tokens(0)
         norm(0)
-        quantise_kn(0)
+        project(1)
         for g in range(n_groups):
             if g + 1 < n_groups:
                 to_tokens(g + 1)
             products(g)
             if g >= 1:
                 main_passes(g - 1)
-            if g >= GROUPS and g % GROUPS == 0:
-                square_up(g // GROUPS - 1)
             if g + 3 < n_groups:
                 load(g + 3)
             if g + 2 < n_groups:
                 turn_x(g + 2)
-                quantise_x(g + 2)
+            if g >= GROUPS and g % GROUPS == 0:
+                square_up(g // GROUPS - 1)
             if g + 1 < n_groups:
                 norm(g + 1)
+            if g + 2 < n_groups:
+                quantise_x(g + 2)
+            quantise_v(g)
             quantise_products(g)
-            if g + 1 < n_groups:
-                quantise_kn(g + 1)
+            quantise_kn(g)
             if g + 2 < n_groups:
                 project(g + 2)
             if g >= GROUPS and g % GROUPS == 0:

@@ -27,7 +27,7 @@ MAIN = 512
 TAIL = 128
 PAIRS = MAIN + TAIL
 ROW_START = {0: 0, 1: 256, 3: 448, 2: 512}
-GPSIMD_ROWS = (1, 3)
+GPSIMD_ROWS = (1,)
 
 FLOPS = 2 * B * N_TOK * C * 2 * H * D + 2 * B * H * N_TOK * D * D * D + 2 * B * H * N_TOK * D * D
 

@@ -23,11 +23,16 @@ EPS = 1e-12
 SCALE_SQ = 32.0**0.5
 BLK = 8
 N_BLK = D // BLK
+HALF = D // 2
 MAIN = 512
-TAIL = 128
-PAIRS = MAIN + TAIL
-ROW_START = {0: 0, 1: 256, 3: 448, 2: 512}
-GPSIMD_ROWS = (1,)
+MID_START = HALF * HALF
+DIAG_START = MID_START + 2 * BLK * BLK
+TAIL_STRIP = 3
+STRIPS = (0, 1, 2, 4, 5, 6)
+STRIP_START = {0: 416, 1: 444, 2: 468, 4: 488, 5: 500, 6: 508}
+TAIL = H * N_BLK * (BLK - 1 - TAIL_STRIP)
+L_PITCH = N_BLK * (D + BLK)
+GPSIMD_HEADS = (0, 1)
 
 FLOPS = 2 * B * N_TOK * C * 2 * H * D + 2 * B * H * N_TOK * D * D * D + 2 * B * H * N_TOK * D * D
 
@@ -98,13 +103,22 @@ def tile_taylorsoftmaxattention_pa_t_kernel(
         for h in range(H):
             own = slice(D * h, D * (h + 1))
             nc.vector.tensor_copy(out=rep_head[own, h, :], in_=rep[own].rearrange("k J i -> k (J i)"))
+        of_head = const.tile([P, H], F32)
+        nc.vector.tensor_reduce(
+            out=of_head[:], in_=ident[:].rearrange("k (h d) -> k h d", h=H), axis=AX.X, op=ALU.add
+        )
         ones = const.tile([P, PACK], F32)
         nc.vector.memset(ones[:], 1.0)
 
-        v_diag = [const.tile([P, H, 640], BF16, name="v_diag%d" % n, align_bytes=64) for n in range(2)]
+        v_mask = [const.tile([P, H, P + D], I32, name="v_mask%d" % n, align_bytes=64) for n in range(3)]
         kn_tok = [const.tile([P, PACK, P + 4], F32, name="kn_tok%d" % n) for n in range(4)]
-        for n in range(2):
-            nc.vector.memset(v_diag[n][:], 0.0)
+        for n in range(3):
+            nc.gpsimd.memset(v_mask[n][:], 0)
+        tail_q = [const.tile([P, P], I32, name="tail_q%d" % n, align_bytes=64) for n in range(3)]
+        tail_s = [const.tile([P, P], U8, name="tail_s%d" % n, align_bytes=64) for n in range(3)]
+        for n in range(3):
+            nc.gpsimd.memset(tail_q[n][:], 0)
+            nc.gpsimd.memset(tail_s[n][:].bitcast(I32), 0)
         for n in range(4):
             nc.scalar.copy(out=kn_tok[n][:, :, P : P + 1], in_=ones[:].unsqueeze(2))
         v_sums = const.tile([P, B * GROUPS], F32)
@@ -154,8 +168,10 @@ def tile_taylorsoftmaxattention_pa_t_kernel(
                     )
                 sums.append(acc)
             kT = work.tile([P, K_PASS], F32, tag="kT")
+            squares = work.tile([P, K_PASS], F32, tag="squares")
             vT = work.tile([P, K_PASS], F32, tag="vT")
             nc.scalar.activation(out=kT[:], in_=sums[0][:], func=ACT.Identity, bias=bias_col[:, 0:1], scale=1.0)
+            nc.scalar.activation(out=squares[:], in_=sums[0][:], func=ACT.Square, bias=bias_col[:, 0:1], scale=1.0)
             nc.scalar.activation(
                 out=vT[:],
                 in_=sums[1][:],
@@ -165,25 +181,49 @@ def tile_taylorsoftmaxattention_pa_t_kernel(
                 accum_out=v_sums[:, g : g + 1],
             )
             held["kT", g] = kT
+            held["squares", g] = squares
             held["vT", g] = vT
 
         def to_tokens(g):
             k_tok = ktok_ps.tile([P, PACK, P], F32, tag="k_tok")
+            sumsq = misc_ps.tile([P, PACK * H], F32, tag="misc", name="sumsq")
             v_tok = turn_ps.tile([P, PACK, P], F32, tag="turn")
             for t in range(PACK):
                 nc.tensor.transpose(k_tok[:, t, :], held["kT", g][:, P * t : P * (t + 1)], ident[:])
             for t in range(PACK):
+                nc.tensor.matmul(
+                    out=sumsq[:, H * t : H * (t + 1)],
+                    lhsT=held["squares", g][:, P * t : P * (t + 1)],
+                    rhs=of_head[:],
+                    start=True,
+                    stop=True,
+                )
+            for t in range(PACK):
                 nc.tensor.transpose(v_tok[:, t, :], held["vT", g][:, P * t : P * (t + 1)], ident[:])
-            squares = work.tile([P, PACK * H, D], F32, tag="squares")
-            nc.scalar.activation(
-                out=squares[:], in_=k_tok[:].rearrange("p t (h d) -> p (t h) d", d=D), func=ACT.Square
-            )
-            nc.scalar.copy(
-                out=v_diag[g % 2][:, :, 0 : D * PACK].rearrange("p h (e t) -> p h e t", t=PACK),
-                in_=v_tok[:].rearrange("p t (h e) -> p h e t", h=H),
-            )
+            v_bf = work.tile([P, P, PACK], BF16, tag="v_bf", align_bytes=64)
+            nc.scalar.copy(out=v_bf[:], in_=v_tok[:].rearrange("p t f -> p f t"))
+            held["v_bf", g] = v_bf
             held["k_tok", g] = k_tok
-            held["squares", g] = squares
+            held["sumsq", g] = sumsq
+
+        def floor_norm(g):
+            floored = work.tile([P, PACK * H], F32, tag="floored")
+            nc.vector.tensor_scalar(
+                out=floored[:],
+                in0=held["sumsq", g][:],
+                scalar1=EPS * EPS,
+                scalar2=1.0 / SCALE_SQ,
+                op0=ALU.max,
+                op1=ALU.mult,
+            )
+            held["floored", g] = floored
+
+        def factors(g):
+            r2 = work.tile([P, PACK * H], F32, tag="r2")
+            nc.vector.reciprocal(out=r2[:], in_=held["floored", g][:])
+            r1 = work.tile([P, PACK * H], F32, tag="r1")
+            nc.scalar.activation(out=r1[:], in_=r2[:], func=ACT.Sqrt)
+            held["r2", g], held["r1", g] = r2, r1
 
         def scale_k(g, factor, tag):
             scaled = work.tile([P, P, PACK], F32, tag=tag, name=tag)
@@ -196,33 +236,26 @@ def tile_taylorsoftmaxattention_pa_t_kernel(
             return scaled
 
         def norm(g):
-            sumsq = work.tile([P, PACK * H], F32, tag="sumsq")
-            nc.vector.tensor_reduce(out=sumsq[:], in_=held["squares", g][:], axis=AX.X, op=ALU.add)
-            floored = work.tile([P, PACK * H], F32, tag="floored")
-            nc.vector.tensor_scalar(
-                out=floored[:], in0=sumsq[:], scalar1=EPS * EPS, scalar2=1.0 / SCALE_SQ, op0=ALU.max, op1=ALU.mult
-            )
-            r2 = work.tile([P, PACK * H], F32, tag="r2")
-            nc.vector.reciprocal(out=r2[:], in_=floored[:])
-            r1 = work.tile([P, PACK * H], F32, tag="r1")
-            nc.scalar.activation(out=r1[:], in_=r2[:], func=ACT.Sqrt)
-            held["k_r2", g] = scale_k(g, r2, "k_r2")
-            kn = scale_k(g, r1, "kn")
+            kn = scale_k(g, held["r1", g], "kn")
             held["kn", g] = kn
+            held["k_r2", g] = scale_k(g, held["r2", g], "k_r2")
             nc.scalar.copy(out=kn_tok[g % 4][:, :, 0:P], in_=kn[:].rearrange("p f t -> p t f"))
             kn_bf = work.tile([P, P * PACK], BF16, tag="kn_bf", align_bytes=64)
             nc.scalar.copy(out=kn_bf[:], in_=kn[:].rearrange("p f t -> p (f t)"))
             held["kn_bf", g] = kn_bf
 
         def quantise_v(g):
-            v_q = words.tile([P, H * P], U32, tag="v_q", align_bytes=64)
-            v_s = words.tile([P, H * P], U8, tag="v_s", align_bytes=64)
+            v_q = words.tile([P, P], I32, tag="v_q", align_bytes=64)
+            v_s = words.tile([P, P], U8, tag="v_s", align_bytes=64)
             nc.vector.quantize_mx(
-                out=v_q[:].bitcast(FP8X4),
-                scales=v_s[:],
-                in_=v_diag[g % 2][:].rearrange("p h x -> p (h x)")[:, 0 : H * P * PACK],
+                out=v_q[:].bitcast(FP8X4), scales=v_s[:], in_=held["v_bf", g][:].rearrange("p f t -> p (f t)")
             )
             held["v_q", g] = (v_q, v_s)
+
+        def mask_v(g):
+            nc.vector.tensor_copy(
+                out=v_mask[g % 3][:, :, 0:D], in_=held["v_q", g][0][:].rearrange("p (h e) -> p h e", h=H)
+            )
 
         def quantise_kn(g):
             kn_q = words.tile([P, P], U32, tag="kn_q", align_bytes=64)
@@ -230,68 +263,105 @@ def tile_taylorsoftmaxattention_pa_t_kernel(
             nc.vector.quantize_mx(out=kn_q[:].bitcast(FP8X4), scales=kn_s[:], in_=held["kn_bf", g][:])
             held["kn_q", g] = (kn_q, kn_s)
 
-        def products(g):
+        def new_products(g):
+            kk_bf = single.tile([P, H, MAIN, PACK], BF16, tag="kk_bf", align_bytes=64)
+            kk_tail = single.tile([P, TAIL, PACK], BF16, tag="kk_tail", align_bytes=64)
+            held["kk_bf", g] = (kk_bf, kk_tail)
+
+        def square_block(g, h, start, i, j, side):
             k_tok, k_r2, kn = held["k_tok", g], held["k_r2", g], held["kn", g]
-            kk_bf = single.tile([P, H, PAIRS, PACK], BF16, tag="kk_bf", align_bytes=64)
+            kk_bf = held["kk_bf", g][0]
+            shape = [P, side, side, PACK]
+            out = kk_bf[:, h, start : start + side * side, :].rearrange("p (i j) t -> p i j t", i=side)
+            rows = slice(D * h + i, D * h + i + side)
+            cols = slice(D * h + j, D * h + j + side)
+            if side == HALF and h in GPSIMD_HEADS:
+                nc.gpsimd.tensor_tensor(
+                    out=out,
+                    in0=kn[:, rows, :].unsqueeze(2).to_broadcast(shape),
+                    in1=kn[:, cols, :].unsqueeze(1).to_broadcast(shape),
+                    op=ALU.mult,
+                )
+            else:
+                nc.vector.tensor_tensor(
+                    out=out,
+                    in0=k_tok[:].rearrange("p t f -> p f t")[:, rows, :].unsqueeze(2).to_broadcast(shape),
+                    in1=k_r2[:, cols, :].unsqueeze(1).to_broadcast(shape),
+                    op=ALU.mult,
+                )
+
+        def large_blocks(g):
             for h in range(H):
-                for row in range(N_BLK):
-                    width = D - BLK * row
-                    first = D * h + BLK * row
-                    shape = [P, BLK, width, PACK]
-                    out = kk_bf[:, h, ROW_START[row] : ROW_START[row] + BLK * width, :].rearrange(
-                        "p (i j) t -> p i j t", i=BLK
+                square_block(g, h, 0, 0, HALF, HALF)
+
+        def small_blocks(g):
+            for h in range(H):
+                for b in range(2):
+                    square_block(g, h, MID_START + BLK * BLK * b, HALF * b, HALF * b + BLK, BLK)
+
+        def diagonal(g):
+            kk_bf, kn = held["kk_bf", g][0], held["kn", g]
+            nc.scalar.activation(
+                out=kk_bf[:, :, DIAG_START : DIAG_START + D, :],
+                in_=kn[:].rearrange("p (h f) t -> p h f t", h=H),
+                func=ACT.Square,
+            )
+
+        def strips(g):
+            k_rows = held["k_tok", g][:].rearrange("p t (h G a) -> p h G a t", h=H, G=N_BLK)
+            k_cols = held["k_r2", g][:].rearrange("p (h G a) t -> p h G a t", h=H, G=N_BLK)
+            kk_bf, kk_tail = held["kk_bf", g]
+            for a in range(BLK - 1):
+                width = BLK - 1 - a
+                shape = [P, H, N_BLK, width, PACK]
+                if a == TAIL_STRIP:
+                    out = kk_tail[:].rearrange("p (h G w) t -> p h G w t", h=H, G=N_BLK)
+                else:
+                    out = kk_bf[:, :, STRIP_START[a] : STRIP_START[a] + N_BLK * width, :].rearrange(
+                        "p h (G w) t -> p h G w t", G=N_BLK
                     )
-                    if row in GPSIMD_ROWS:
-                        nc.gpsimd.tensor_tensor(
-                            out=out,
-                            in0=kn[:, first : first + BLK, :].unsqueeze(2).to_broadcast(shape),
-                            in1=kn[:, first : first + width, :].unsqueeze(1).to_broadcast(shape),
-                            op=ALU.mult,
-                        )
-                    else:
-                        nc.vector.tensor_tensor(
-                            out=out,
-                            in0=k_tok[:, :, first : first + BLK]
-                            .rearrange("p t i -> p i t")
-                            .unsqueeze(2)
-                            .to_broadcast(shape),
-                            in1=k_r2[:, first : first + width, :].unsqueeze(1).to_broadcast(shape),
-                            op=ALU.mult,
-                        )
-            held["kk_bf", g] = kk_bf
+                nc.vector.tensor_tensor(
+                    out=out,
+                    in0=k_rows[:, :, :, a : a + 1, :].to_broadcast(shape),
+                    in1=k_cols[:, :, :, a + 1 : BLK, :],
+                    op=ALU.mult,
+                )
 
         def quantise_products(g):
-            kk_bf = held["kk_bf", g]
-            kk_q = words.tile([P, H, PAIRS], U32, tag="kk_q", align_bytes=64)
-            kk_s = words.tile([P, H, PAIRS], U8, tag="kk_s", align_bytes=64)
+            kk_bf, kk_tail = held["kk_bf", g]
+            kk_q = words.tile([P, H, MAIN], U32, tag="kk_q", align_bytes=64)
+            kk_s = words.tile([P, H, MAIN], U8, tag="kk_s", align_bytes=64)
             for h in range(H):
-                for cols in (slice(0, MAIN), slice(MAIN, PAIRS)):
-                    nc.vector.quantize_mx(
-                        out=kk_q[:, h, cols].bitcast(FP8X4),
-                        scales=kk_s[:, h, cols],
-                        in_=kk_bf[:, h, cols, :].rearrange("p c t -> p (c t)"),
-                    )
-            held["kk_q", g] = (kk_q, kk_s)
-
-        def moment_passes(out, g, cols):
-            v_q, v_s = held["v_q", g]
-            kk_q, kk_s = held["kk_q", g]
-            for h in range(H):
-                nc.tensor.matmul_mx(
-                    out=out,
-                    lhsT=v_q[:, P * h : P * (h + 1)].bitcast(FP8X4),
-                    lhsT_scale=v_s[:, P * h : P * (h + 1)],
-                    rhs=kk_q[:, h, cols].bitcast(FP8X4),
-                    rhs_scale=kk_s[:, h, cols],
-                    start=(g % GROUPS == 0 and h == 0),
-                    stop=(g % GROUPS == GROUPS - 1 and h == H - 1),
+                nc.vector.quantize_mx(
+                    out=kk_q[:, h, :].bitcast(FP8X4),
+                    scales=kk_s[:, h, :],
+                    in_=kk_bf[:, h, :, :].rearrange("p c t -> p (c t)"),
                 )
+            nc.vector.quantize_mx(
+                out=tail_q[g % 3][:, 0:TAIL].bitcast(FP8X4),
+                scales=tail_s[g % 3][:, 0:TAIL],
+                in_=kk_tail[:].rearrange("p c t -> p (c t)"),
+            )
+            held["kk_q", g] = (kk_q, kk_s)
 
         def main_passes(g):
             if g % GROUPS == 0:
                 z_main = main_ps.tile([P, MAIN], F32, tag="z_main")
                 held["z_main", g // GROUPS] = z_main
-            moment_passes(held["z_main", g // GROUPS][:], g, slice(0, MAIN))
+            z_main = held["z_main", g // GROUPS]
+            v_masked = v_mask[g % 3][:].rearrange("p h x -> p (h x)")
+            v_s = held["v_q", g][1]
+            kk_q, kk_s = held["kk_q", g]
+            for h in range(H):
+                nc.tensor.matmul_mx(
+                    out=z_main[:],
+                    lhsT=v_masked[:, P * h : P * (h + 1)].bitcast(FP8X4),
+                    lhsT_scale=v_s[:],
+                    rhs=kk_q[:, h, :].bitcast(FP8X4),
+                    rhs_scale=kk_s[:, h, :],
+                    start=(g % GROUPS == 0 and h == 0),
+                    stop=(g % GROUPS == GROUPS - 1 and h == H - 1),
+                )
 
         def float_sums(b):
             o_tile = work.tile([P, H, BLK, D + 1], F32, tag="o_tile")
@@ -323,54 +393,82 @@ def tile_taylorsoftmaxattention_pa_t_kernel(
                     in_=q[rows, :].rearrange("p (h j) -> p h j", h=H)[:, :, BLK * J : BLK * (J + 1)].unsqueeze(3),
                 )
 
-        def spread(z_sq, bank, row):
-            width = D - BLK * row
-            start = ROW_START[row] % MAIN
-            block_row = bank[:, start : start + BLK * width]
-            nc.scalar.copy(
-                out=z_sq[:, :, row:N_BLK, BLK * row : BLK * (row + 1)],
-                in_=block_row.rearrange("p (a J l) -> p l J a", a=BLK, l=BLK),
-            )
-            if width > BLK:
-                nc.scalar.copy(
-                    out=z_sq[:, :, row, BLK * (row + 1) : D],
-                    in_=block_row.rearrange("p (a j) -> p a j", a=BLK)[:, :, BLK:width],
-                )
-
         def square_up(b):
-            z_tail = misc_ps.tile([P, TAIL], F32, tag="misc")
+            z_tail = misc_ps.tile([P, P], F32, tag="misc")
             for part in range(GROUPS):
-                moment_passes(z_tail[:], GROUPS * b + part, slice(MAIN, PAIRS))
-            z_sq = work.tile([P, BLK, N_BLK, D], F32, tag="z_sq")
-            for row in range(N_BLK):
-                spread(z_sq, held["z_main", b] if ROW_START[row] < MAIN else z_tail, row)
-            held["z_sq", b] = z_sq
+                g = GROUPS * b + part
+                v_q, v_s = held["v_q", g]
+                nc.tensor.matmul_mx(
+                    out=z_tail[:],
+                    lhsT=v_q[:].bitcast(FP8X4),
+                    lhsT_scale=v_s[:],
+                    rhs=tail_q[g % 3][:].bitcast(FP8X4),
+                    rhs_scale=tail_s[g % 3][:],
+                    start=(part == 0),
+                    stop=(part == GROUPS - 1),
+                )
+            tail_sb = work.tile([P, TAIL // H], F32, tag="tail_sb")
+            for h in range(H):
+                own = slice(D * h, D * (h + 1))
+                nc.scalar.copy(out=tail_sb[own, :], in_=z_tail[own, TAIL // H * h : TAIL // H * (h + 1)])
+            z_main = held["z_main", b]
+            z_sq = work.tile([P, BLK * L_PITCH + BLK], F32, tag="z_sq")
+            rows = z_sq[:, 0 : BLK * L_PITCH].rearrange("p (l x) -> p l x", l=BLK)
+            square = rows[:, :, 0:P].rearrange("p l (J i) -> p l J i", J=N_BLK)
+            middle = rows.rearrange("p l (b x) -> p l b x", b=2)
+            diagonal = rows.rearrange("p l (G x) -> p l G x", G=N_BLK)
 
-        def outputs(b):
-            o_tile, kv_tile, z_sq = held["o_tile", b], held["kv_tile", b], held["z_sq", b]
+            z = z_main[:, 0:MID_START]
+            nc.scalar.copy(out=square[:, :, 2:4, 0:HALF], in_=z.rearrange("p (i J l) -> p l J i", J=2, l=BLK))
+            nc.scalar.copy(out=square[:, :, 0:2, HALF:D], in_=z.rearrange("p (J l j) -> p l J j", J=2, l=BLK))
+            z = z_main[:, MID_START:DIAG_START]
+            nc.scalar.copy(
+                out=middle[:, :, :, D : D + BLK], in_=z.rearrange("p (b a l) -> p l b a", b=2, l=BLK)
+            )
+            nc.scalar.copy(
+                out=middle[:, :, :, BLK : 2 * BLK], in_=z.rearrange("p (b l c) -> p l b c", b=2, l=BLK)
+            )
+            nc.scalar.copy(
+                out=z_sq[:].rearrange("p (a x) -> p a x", a=BLK)[:, :, 0:L_PITCH].rearrange(
+                    "p a (G x) -> p a G x", G=N_BLK
+                )[:, :, :, 0],
+                in_=z_main[:, DIAG_START : DIAG_START + D].rearrange("p (G a) -> p a G", G=N_BLK),
+            )
+            for a in range(BLK - 1):
+                width = BLK - 1 - a
+                z = tail_sb[:] if a == TAIL_STRIP else z_main[:, STRIP_START[a] : STRIP_START[a] + N_BLK * width]
+                z = z.rearrange("p (G w) -> p G w", G=N_BLK)
+                nc.scalar.copy(out=diagonal[:, a + 1 : BLK, :, a].rearrange("p w G -> p G w"), in_=z)
+                nc.scalar.copy(out=diagonal[:, a, :, a + 1 : BLK], in_=z)
+            held["z_sq", b] = rows
+
+        def kv_out(b):
+            kv_tile = held["kv_tile", b]
             kv_ps = misc_ps.tile([P, P], F32, tag="misc")
             for part in range(GROUPS):
                 v_q, v_s = held["v_q", GROUPS * b + part]
                 kn_q, kn_s = held["kn_q", GROUPS * b + part]
-                for h in range(H):
-                    nc.tensor.matmul_mx(
-                        out=kv_ps[:],
-                        lhsT=kn_q[:].bitcast(FP8X4),
-                        lhsT_scale=kn_s[:],
-                        rhs=v_q[:, P * h : P * (h + 1)].bitcast(FP8X4),
-                        rhs_scale=v_s[:, P * h : P * (h + 1)],
-                        start=(part == 0 and h == 0),
-                        stop=(part == GROUPS - 1 and h == H - 1),
-                    )
+                nc.tensor.matmul_mx(
+                    out=kv_ps[:],
+                    lhsT=kn_q[:].bitcast(FP8X4),
+                    lhsT_scale=kn_s[:],
+                    rhs=v_q[:].bitcast(FP8X4),
+                    rhs_scale=v_s[:],
+                    start=(part == 0),
+                    stop=(part == GROUPS - 1),
+                )
             for h in range(H):
                 own = slice(D * h, D * (h + 1))
                 nc.scalar.copy(out=kv_tile[own, 1 : D + 1], in_=kv_ps[own, own])
             nc.scalar.dma_start(out=out_1[b].rearrange("h d c -> (h d) c"), in_=kv_tile[:])
+
+        def kv_mod_out(b):
+            o_tile, z_sq = held["o_tile", b], held["z_sq", b]
             for half in range(2):
                 turned = turn_ps.tile([P, PACK, P], F32, tag="turn")
                 for n in range(PACK):
                     nc.tensor.transpose(
-                        turned[:, n, :], z_sq[:, PACK * half + n, :, :].rearrange("p J i -> p (J i)"), ident[:]
+                        turned[:, n, :], z_sq[:, PACK * half + n, 0:P], ident[:]
                     )
                 nc.scalar.copy(
                     out=o_tile[:, :, PACK * half : PACK * (half + 1), 1 : D + 1],
@@ -395,20 +493,30 @@ def tile_taylorsoftmaxattention_pa_t_kernel(
         quantise_x(1)
         project(0)
         to_tokens(0)
+        floor_norm(0)
+        factors(0)
         norm(0)
         project(1)
         for g in range(n_groups):
+            last_of_batch = g % GROUPS == GROUPS - 1
+            done = g // GROUPS - 1
             if g + 1 < n_groups:
                 to_tokens(g + 1)
-            products(g)
+            new_products(g)
+            large_blocks(g)
+            if g + 1 < n_groups:
+                floor_norm(g + 1)
+            small_blocks(g)
+            if g + 1 < n_groups:
+                factors(g + 1)
+            diagonal(g)
             if g >= 1:
                 main_passes(g - 1)
             if g + 3 < n_groups:
                 load(g + 3)
             if g + 2 < n_groups:
                 turn_x(g + 2)
-            if g >= GROUPS and g % GROUPS == 0:
-                square_up(g // GROUPS - 1)
+            strips(g)
             if g + 1 < n_groups:
                 norm(g + 1)
             if g + 2 < n_groups:
@@ -416,15 +524,21 @@ def tile_taylorsoftmaxattention_pa_t_kernel(
             quantise_v(g)
             quantise_products(g)
             quantise_kn(g)
+            mask_v(g)
+            if last_of_batch:
+                float_sums(g // GROUPS)
             if g + 2 < n_groups:
                 project(g + 2)
-            if g >= GROUPS and g % GROUPS == 0:
-                outputs(g // GROUPS - 1)
-            if g % GROUPS == GROUPS - 1:
-                float_sums(g // GROUPS)
+            if done >= 0:
+                if last_of_batch:
+                    kv_mod_out(done)
+                else:
+                    square_up(done)
+                    kv_out(done)
         main_passes(n_groups - 1)
         square_up(B - 1)
-        outputs(B - 1)
+        kv_out(B - 1)
+        kv_mod_out(B - 1)
 
         sums_sq = const.tile([P, P], F32)
         nc.vector.memset(sums_sq[:], 0.0)

@@ -43,7 +43,7 @@ def tile_taylorsoftmaxattention_pa_t_kernel(
     nc = tc.nc
     with ExitStack() as ctx:
         const = ctx.enter_context(tc.tile_pool(name="const", bufs=1))
-        x_pool = ctx.enter_context(tc.tile_pool(name="x_pool", bufs=3))
+        x_pool = ctx.enter_context(tc.tile_pool(name="x_pool", bufs=4))
         work = ctx.enter_context(tc.tile_pool(name="work", bufs=2))
         words = ctx.enter_context(tc.tile_pool(name="words", bufs=3))
         single = ctx.enter_context(tc.tile_pool(name="single", bufs=1))
@@ -92,6 +92,7 @@ def tile_taylorsoftmaxattention_pa_t_kernel(
         nc.sync.dma_start(out=bias_rows[1:2, :], in_=bv.unsqueeze(0))
         load(1)
         load(2)
+        load(3)
         rep_one = const.tile([P, D], F32)
         nc.vector.tensor_reduce(
             out=rep_one[:], in_=ident[:].rearrange("k (h i) -> k i h", h=H), axis=AX.X, op=ALU.add
@@ -123,26 +124,27 @@ def tile_taylorsoftmaxattention_pa_t_kernel(
             nc.scalar.copy(out=kn_tok[n][:, :, P : P + 1], in_=ones[:].unsqueeze(2))
         v_sums = const.tile([P, B * GROUPS], F32)
 
-        def turn_x(g):
+        def turn_x(g, quarters):
             xs = held["xs", g]
-            x_grouped = work.tile([P, C_PASSES * K_PASS * PACK], BF16, tag="x_grouped", align_bytes=64)
-            grouped_words = x_grouped[:].bitcast(F32).rearrange("p (c n u) -> p c n u", c=C_PASSES, u=2)
-            for c in range(C_PASSES):
-                for half in range(2):
-                    turned = turn_ps.tile([P, 2, 2 * P], F32, tag="turn")
-                    for u in range(2):
-                        for tl in range(2):
-                            x_words = xs[:, 2 * half + tl, :].bitcast(F32)
-                            nc.tensor.transpose(
-                                turned[:, u, P * tl : P * (tl + 1)],
-                                x_words[:, 256 * c + u : 256 * (c + 1) : 2],
-                                ident[:],
-                            )
-                    nc.scalar.copy(
-                        out=grouped_words[:, c, 2 * P * half : 2 * P * (half + 1), :],
-                        in_=turned[:].rearrange("p u n -> p n u"),
-                    )
-            held["x_grouped", g] = x_grouped
+            if 0 in quarters:
+                x_grouped = work.tile([P, C_PASSES * K_PASS * PACK], BF16, tag="x_grouped", align_bytes=64)
+                held["x_grouped", g] = x_grouped
+            grouped_words = held["x_grouped", g][:].bitcast(F32).rearrange("p (c n u) -> p c n u", c=C_PASSES, u=2)
+            for quarter in quarters:
+                c, half = divmod(quarter, 2)
+                turned = turn_ps.tile([P, 2, 2 * P], F32, tag="turn")
+                for u in range(2):
+                    for tl in range(2):
+                        x_words = xs[:, 2 * half + tl, :].bitcast(F32)
+                        nc.tensor.transpose(
+                            turned[:, u, P * tl : P * (tl + 1)],
+                            x_words[:, 256 * c + u : 256 * (c + 1) : 2],
+                            ident[:],
+                        )
+                nc.scalar.copy(
+                    out=grouped_words[:, c, 2 * P * half : 2 * P * (half + 1), :],
+                    in_=turned[:].rearrange("p u n -> p n u"),
+                )
 
         def quantise_x(g):
             x_q = work.tile([P, C_PASSES * K_PASS], U32, tag="x_q", align_bytes=64)
@@ -184,12 +186,14 @@ def tile_taylorsoftmaxattention_pa_t_kernel(
             held["squares", g] = squares
             held["vT", g] = vT
 
-        def to_tokens(g):
+        def k_to_tokens(g):
             k_tok = ktok_ps.tile([P, PACK, P], F32, tag="k_tok")
-            sumsq = misc_ps.tile([P, PACK * H], F32, tag="misc", name="sumsq")
-            v_tok = turn_ps.tile([P, PACK, P], F32, tag="turn")
             for t in range(PACK):
                 nc.tensor.transpose(k_tok[:, t, :], held["kT", g][:, P * t : P * (t + 1)], ident[:])
+            held["k_tok", g] = k_tok
+
+        def sum_squares(g):
+            sumsq = misc_ps.tile([P, PACK * H], F32, tag="misc", name="sumsq")
             for t in range(PACK):
                 nc.tensor.matmul(
                     out=sumsq[:, H * t : H * (t + 1)],
@@ -198,13 +202,15 @@ def tile_taylorsoftmaxattention_pa_t_kernel(
                     start=True,
                     stop=True,
                 )
+            held["sumsq", g] = sumsq
+
+        def v_to_tokens(g):
+            v_tok = turn_ps.tile([P, PACK, P], F32, tag="turn", name="v_tok")
             for t in range(PACK):
                 nc.tensor.transpose(v_tok[:, t, :], held["vT", g][:, P * t : P * (t + 1)], ident[:])
             v_bf = work.tile([P, P, PACK], BF16, tag="v_bf", align_bytes=64)
             nc.scalar.copy(out=v_bf[:], in_=v_tok[:].rearrange("p t f -> p f t"))
             held["v_bf", g] = v_bf
-            held["k_tok", g] = k_tok
-            held["sumsq", g] = sumsq
 
         def floor_norm(g):
             floored = work.tile([P, PACK * H], F32, tag="floored")
@@ -239,7 +245,10 @@ def tile_taylorsoftmaxattention_pa_t_kernel(
             kn = scale_k(g, held["r1", g], "kn")
             held["kn", g] = kn
             held["k_r2", g] = scale_k(g, held["r2", g], "k_r2")
-            nc.scalar.copy(out=kn_tok[g % 4][:, :, 0:P], in_=kn[:].rearrange("p f t -> p t f"))
+
+        def copy_kn(g):
+            kn = held["kn", g]
+            nc.scalar.copy(out=kn_tok[g % 4][:, :, 0:P].rearrange("p t f -> p f t"), in_=kn[:])
             kn_bf = work.tile([P, P * PACK], BF16, tag="kn_bf", align_bytes=64)
             nc.scalar.copy(out=kn_bf[:], in_=kn[:].rearrange("p f t -> p (f t)"))
             held["kn_bf", g] = kn_bf
@@ -290,12 +299,12 @@ def tile_taylorsoftmaxattention_pa_t_kernel(
                     op=ALU.mult,
                 )
 
-        def large_blocks(g):
-            for h in range(H):
+        def large_blocks(g, heads):
+            for h in heads:
                 square_block(g, h, 0, 0, HALF, HALF)
 
-        def small_blocks(g):
-            for h in range(H):
+        def small_blocks(g, heads):
+            for h in heads:
                 for b in range(2):
                     square_block(g, h, MID_START + BLK * BLK * b, HALF * b, HALF * b + BLK, BLK)
 
@@ -344,15 +353,15 @@ def tile_taylorsoftmaxattention_pa_t_kernel(
             )
             held["kk_q", g] = (kk_q, kk_s)
 
-        def main_passes(g):
-            if g % GROUPS == 0:
+        def main_passes(g, heads):
+            if g % GROUPS == 0 and 0 in heads:
                 z_main = main_ps.tile([P, MAIN], F32, tag="z_main")
                 held["z_main", g // GROUPS] = z_main
             z_main = held["z_main", g // GROUPS]
             v_masked = v_mask[g % 3][:].rearrange("p h x -> p (h x)")
             v_s = held["v_q", g][1]
             kk_q, kk_s = held["kk_q", g]
-            for h in range(H):
+            for h in heads:
                 nc.tensor.matmul_mx(
                     out=z_main[:],
                     lhsT=v_masked[:, P * h : P * (h + 1)].bitcast(FP8X4),
@@ -382,6 +391,10 @@ def tile_taylorsoftmaxattention_pa_t_kernel(
             mn_sb = work.tile([P, P + 1], F32, tag="mn_sb")
             nc.scalar.mul(out=mn_sb[:], in_=mn[:], mul=1.0 / N_TOK)
             nc.scalar.copy(out=kv_tile[:, 0:1], in_=mn_sb[:, P : P + 1])
+            held["mn_sb", b] = mn_sb
+
+        def float_columns(b):
+            mn_sb, o_tile = held["mn_sb", b], held["o_tile", b]
             q = misc_ps.tile([P, P], F32, tag="misc")
             for h in range(H):
                 own = slice(D * h, D * (h + 1))
@@ -393,13 +406,13 @@ def tile_taylorsoftmaxattention_pa_t_kernel(
                     in_=q[rows, :].rearrange("p (h j) -> p h j", h=H)[:, :, BLK * J : BLK * (J + 1)].unsqueeze(3),
                 )
 
-        def square_up(b):
-            z_tail = misc_ps.tile([P, P], F32, tag="misc")
+        def tail_and_kv(b):
+            sums = misc_ps.tile([P, 2, P], F32, tag="misc", name="tail_and_kv_sums")
             for part in range(GROUPS):
                 g = GROUPS * b + part
                 v_q, v_s = held["v_q", g]
                 nc.tensor.matmul_mx(
-                    out=z_tail[:],
+                    out=sums[:, 0, :],
                     lhsT=v_q[:].bitcast(FP8X4),
                     lhsT_scale=v_s[:],
                     rhs=tail_q[g % 3][:].bitcast(FP8X4),
@@ -407,17 +420,34 @@ def tile_taylorsoftmaxattention_pa_t_kernel(
                     start=(part == 0),
                     stop=(part == GROUPS - 1),
                 )
+            for part in range(GROUPS):
+                g = GROUPS * b + part
+                v_q, v_s = held["v_q", g]
+                kn_q, kn_s = held["kn_q", g]
+                nc.tensor.matmul_mx(
+                    out=sums[:, 1, :],
+                    lhsT=kn_q[:].bitcast(FP8X4),
+                    lhsT_scale=kn_s[:],
+                    rhs=v_q[:].bitcast(FP8X4),
+                    rhs_scale=v_s[:],
+                    start=(part == 0),
+                    stop=(part == GROUPS - 1),
+                )
             tail_sb = work.tile([P, TAIL // H], F32, tag="tail_sb")
+            kv_tile = held["kv_tile", b]
             for h in range(H):
                 own = slice(D * h, D * (h + 1))
-                nc.scalar.copy(out=tail_sb[own, :], in_=z_tail[own, TAIL // H * h : TAIL // H * (h + 1)])
+                nc.scalar.copy(out=tail_sb[own, :], in_=sums[own, 0, TAIL // H * h : TAIL // H * (h + 1)])
+                nc.scalar.copy(out=kv_tile[own, 1 : D + 1], in_=sums[own, 1, own])
+            nc.sync.dma_start(out=out_1[b].rearrange("h d c -> (h d) c"), in_=kv_tile[:])
+            held["tail_sb", b] = tail_sb
+
+        def spread_blocks(b):
             z_main = held["z_main", b]
             z_sq = work.tile([P, BLK * L_PITCH + BLK], F32, tag="z_sq")
             rows = z_sq[:, 0 : BLK * L_PITCH].rearrange("p (l x) -> p l x", l=BLK)
             square = rows[:, :, 0:P].rearrange("p l (J i) -> p l J i", J=N_BLK)
             middle = rows.rearrange("p l (b x) -> p l b x", b=2)
-            diagonal = rows.rearrange("p l (G x) -> p l G x", G=N_BLK)
-
             z = z_main[:, 0:MID_START]
             nc.scalar.copy(out=square[:, :, 2:4, 0:HALF], in_=z.rearrange("p (i J l) -> p l J i", J=2, l=BLK))
             nc.scalar.copy(out=square[:, :, 0:2, HALF:D], in_=z.rearrange("p (J l j) -> p l J j", J=2, l=BLK))
@@ -434,33 +464,17 @@ def tile_taylorsoftmaxattention_pa_t_kernel(
                 )[:, :, :, 0],
                 in_=z_main[:, DIAG_START : DIAG_START + D].rearrange("p (G a) -> p a G", G=N_BLK),
             )
+            held["z_sq", b] = rows
+
+        def spread_strips(b):
+            z_main, tail_sb = held["z_main", b], held["tail_sb", b]
+            diagonal = held["z_sq", b].rearrange("p l (G x) -> p l G x", G=N_BLK)
             for a in range(BLK - 1):
                 width = BLK - 1 - a
                 z = tail_sb[:] if a == TAIL_STRIP else z_main[:, STRIP_START[a] : STRIP_START[a] + N_BLK * width]
                 z = z.rearrange("p (G w) -> p G w", G=N_BLK)
                 nc.scalar.copy(out=diagonal[:, a + 1 : BLK, :, a].rearrange("p w G -> p G w"), in_=z)
                 nc.scalar.copy(out=diagonal[:, a, :, a + 1 : BLK], in_=z)
-            held["z_sq", b] = rows
-
-        def kv_out(b):
-            kv_tile = held["kv_tile", b]
-            kv_ps = misc_ps.tile([P, P], F32, tag="misc")
-            for part in range(GROUPS):
-                v_q, v_s = held["v_q", GROUPS * b + part]
-                kn_q, kn_s = held["kn_q", GROUPS * b + part]
-                nc.tensor.matmul_mx(
-                    out=kv_ps[:],
-                    lhsT=kn_q[:].bitcast(FP8X4),
-                    lhsT_scale=kn_s[:],
-                    rhs=v_q[:].bitcast(FP8X4),
-                    rhs_scale=v_s[:],
-                    start=(part == 0),
-                    stop=(part == GROUPS - 1),
-                )
-            for h in range(H):
-                own = slice(D * h, D * (h + 1))
-                nc.scalar.copy(out=kv_tile[own, 1 : D + 1], in_=kv_ps[own, own])
-            nc.scalar.dma_start(out=out_1[b].rearrange("h d c -> (h d) c"), in_=kv_tile[:])
 
         def kv_mod_out(b):
             o_tile, z_sq = held["o_tile", b], held["z_sq", b]
@@ -475,13 +489,12 @@ def tile_taylorsoftmaxattention_pa_t_kernel(
                     in_=turned[:].rearrange("p l (h e) -> p h l e", h=H),
                 )
             for J in range(N_BLK):
-                nc.scalar.dma_start(
+                nc.sync.dma_start(
                     out=out_0[b, :, :, BLK * J : BLK * (J + 1), :].rearrange("h i l c -> i h (l c)"),
                     in_=o_tile[D * J : D * (J + 1)].rearrange("p h l c -> p h (l c)"),
                 )
 
-        turn_x(0)
-        turn_x(1)
+        turn_x(0, (0, 1, 2, 3))
         bias_rows_f = const.tile([P, P], F32)
         nc.vector.tensor_copy(out=bias_rows_f[:], in_=bias_rows[:])
         bias_ps = turn_ps.tile([P, P], F32, tag="turn")
@@ -490,54 +503,78 @@ def tile_taylorsoftmaxattention_pa_t_kernel(
         nc.scalar.copy(out=bias_col[:, 0:1], in_=bias_ps[:, 0:1])
         nc.scalar.mul(out=bias_col[:, 1:2], in_=bias_ps[:, 1:2], mul=1.0 / N_TOK)
         quantise_x(0)
-        quantise_x(1)
+        turn_x(1, (0, 1, 2, 3))
         project(0)
-        to_tokens(0)
+        sum_squares(0)
+        k_to_tokens(0)
+        quantise_x(1)
         floor_norm(0)
         factors(0)
         norm(0)
         project(1)
+        turn_x(2, (0, 1, 2, 3))
+        v_to_tokens(0)
+        copy_kn(0)
+        quantise_x(2)
+        sum_squares(1)
         for g in range(n_groups):
             last_of_batch = g % GROUPS == GROUPS - 1
             done = g // GROUPS - 1
-            if g + 1 < n_groups:
-                to_tokens(g + 1)
-            new_products(g)
-            large_blocks(g)
-            if g + 1 < n_groups:
+            following = g + 1 < n_groups
+            if following:
+                k_to_tokens(g + 1)
                 floor_norm(g + 1)
-            small_blocks(g)
-            if g + 1 < n_groups:
+            new_products(g)
+            large_blocks(g, (0, 1, 2))
+            if following:
                 factors(g + 1)
+            large_blocks(g, (3,))
             diagonal(g)
-            if g >= 1:
-                main_passes(g - 1)
             if g + 3 < n_groups:
-                load(g + 3)
+                turn_x(g + 3, (0, 1))
+            if g >= 1:
+                main_passes(g - 1, (0, 1))
+            if g + 3 < n_groups:
+                turn_x(g + 3, (2,))
+            if g >= 1:
+                main_passes(g - 1, (2, 3))
+            if g + 3 < n_groups:
+                turn_x(g + 3, (3,))
+            small_blocks(g, (0, 1, 2, 3))
             if g + 2 < n_groups:
-                turn_x(g + 2)
-            strips(g)
-            if g + 1 < n_groups:
+                project(g + 2)
+            if following:
+                v_to_tokens(g + 1)
+            if done >= 0 and not last_of_batch:
+                tail_and_kv(done)
+            if last_of_batch:
+                float_sums(g // GROUPS)
+            if following:
                 norm(g + 1)
-            if g + 2 < n_groups:
-                quantise_x(g + 2)
+            if g + 4 < n_groups:
+                load(g + 4)
+            if following:
+                copy_kn(g + 1)
+            if last_of_batch:
+                float_columns(g // GROUPS)
+            strips(g)
+            if g + 3 < n_groups:
+                quantise_x(g + 3)
             quantise_v(g)
             quantise_products(g)
             quantise_kn(g)
             mask_v(g)
-            if last_of_batch:
-                float_sums(g // GROUPS)
+            if done >= 0 and not last_of_batch:
+                spread_blocks(done)
+                spread_strips(done)
+            if done >= 0 and last_of_batch:
+                kv_mod_out(done)
             if g + 2 < n_groups:
-                project(g + 2)
-            if done >= 0:
-                if last_of_batch:
-                    kv_mod_out(done)
-                else:
-                    square_up(done)
-                    kv_out(done)
-        main_passes(n_groups - 1)
-        square_up(B - 1)
-        kv_out(B - 1)
+                sum_squares(g + 2)
+        main_passes(n_groups - 1, (0, 1, 2, 3))
+        tail_and_kv(B - 1)
+        spread_blocks(B - 1)
+        spread_strips(B - 1)
         kv_mod_out(B - 1)
 
         sums_sq = const.tile([P, P], F32)

@@ -32,7 +32,7 @@ STRIPS = (0, 1, 2, 4, 5, 6)
 STRIP_START = {0: 416, 1: 444, 2: 468, 4: 488, 5: 500, 6: 508}
 TAIL = H * N_BLK * (BLK - 1 - TAIL_STRIP)
 L_PITCH = N_BLK * (D + BLK)
-GPSIMD_HEADS = (0, 1)
+GPSIMD_HEADS = (0, 1, 2)
 
 FLOPS = 2 * B * N_TOK * C * 2 * H * D + 2 * B * H * N_TOK * D * D * D + 2 * B * H * N_TOK * D * D
 

@@ -31,6 +31,7 @@ TAIL_STRIP = 3
 STRIPS = (0, 1, 2, 4, 5, 6)
 STRIP_START = {0: 416, 1: 444, 2: 468, 4: 488, 5: 500, 6: 508}
 TAIL = H * N_BLK * (BLK - 1 - TAIL_STRIP)
+X_AHEAD = 6
 L_PITCH = N_BLK * (D + BLK)
 GPSIMD_HEADS = (0, 1, 2)
 
@@ -43,12 +44,11 @@ def tile_taylorsoftmaxattention_pa_t_kernel(
     nc = tc.nc
     with ExitStack() as ctx:
         const = ctx.enter_context(tc.tile_pool(name="const", bufs=1))
-        x_pool = ctx.enter_context(tc.tile_pool(name="x_pool", bufs=4))
+        x_pool = ctx.enter_context(tc.tile_pool(name="x_pool", bufs=6))
         work = ctx.enter_context(tc.tile_pool(name="work", bufs=2))
         words = ctx.enter_context(tc.tile_pool(name="words", bufs=3))
         single = ctx.enter_context(tc.tile_pool(name="single", bufs=1))
-        turn_ps = ctx.enter_context(tc.psum_pool(name="turn_ps", bufs=2))
-        proj_ps = ctx.enter_context(tc.psum_pool(name="proj_ps", bufs=2))
+        turn_ps = ctx.enter_context(tc.psum_pool(name="turn_ps", bufs=4))
         ktok_ps = ctx.enter_context(tc.psum_pool(name="ktok_ps", bufs=2))
         main_ps = ctx.enter_context(tc.psum_pool(name="main_ps", bufs=1))
         misc_ps = ctx.enter_context(tc.psum_pool(name="misc_ps", bufs=1))
@@ -92,7 +92,8 @@ def tile_taylorsoftmaxattention_pa_t_kernel(
         nc.sync.dma_start(out=bias_rows[1:2, :], in_=bv.unsqueeze(0))
         load(1)
         load(2)
-        load(3)
+        for g in range(3, X_AHEAD):
+            load(g)
         rep_one = const.tile([P, D], F32)
         nc.vector.tensor_reduce(
             out=rep_one[:], in_=ident[:].rearrange("k (h i) -> k i h", h=H), axis=AX.X, op=ALU.add
@@ -156,7 +157,7 @@ def tile_taylorsoftmaxattention_pa_t_kernel(
             x_q, x_s = held["x_q", g]
             sums = []
             for w in range(2):
-                acc = proj_ps.tile([P, K_PASS], F32, tag="proj")
+                acc = turn_ps.tile([P, K_PASS], F32, tag="turn", name="acc")
                 for c in range(C_PASSES):
                     cols = slice(K_PASS * c, K_PASS * (c + 1))
                     nc.tensor.matmul_mx(
@@ -193,7 +194,7 @@ def tile_taylorsoftmaxattention_pa_t_kernel(
             held["k_tok", g] = k_tok
 
         def sum_squares(g):
-            sumsq = misc_ps.tile([P, PACK * H], F32, tag="misc", name="sumsq")
+            sumsq = turn_ps.tile([P, PACK * H], F32, tag="turn", name="sumsq")
             for t in range(PACK):
                 nc.tensor.matmul(
                     out=sumsq[:, H * t : H * (t + 1)],
@@ -227,9 +228,12 @@ def tile_taylorsoftmaxattention_pa_t_kernel(
         def factors(g):
             r2 = work.tile([P, PACK * H], F32, tag="r2")
             nc.vector.reciprocal(out=r2[:], in_=held["floored", g][:])
+            held["r2", g] = r2
+
+        def root(g):
             r1 = work.tile([P, PACK * H], F32, tag="r1")
-            nc.scalar.activation(out=r1[:], in_=r2[:], func=ACT.Sqrt)
-            held["r2", g], held["r1", g] = r2, r1
+            nc.scalar.activation(out=r1[:], in_=held["r2", g][:], func=ACT.Sqrt)
+            held["r1", g] = r1
 
         def scale_k(g, factor, tag):
             scaled = work.tile([P, P, PACK], F32, tag=tag, name=tag)
@@ -336,22 +340,26 @@ def tile_taylorsoftmaxattention_pa_t_kernel(
                     op=ALU.mult,
                 )
 
-        def quantise_products(g):
-            kk_bf, kk_tail = held["kk_bf", g]
-            kk_q = words.tile([P, H, MAIN], U32, tag="kk_q", align_bytes=64)
-            kk_s = words.tile([P, H, MAIN], U8, tag="kk_s", align_bytes=64)
-            for h in range(H):
+        def quantise_tail(g):
+            nc.vector.quantize_mx(
+                out=tail_q[g % 3][:, 0:TAIL].bitcast(FP8X4),
+                scales=tail_s[g % 3][:, 0:TAIL],
+                in_=held["kk_bf", g][1][:].rearrange("p c t -> p (c t)"),
+            )
+
+        def quantise_products(g, heads):
+            if ("kk_q", g) not in held:
+                kk_q = words.tile([P, H, MAIN], U32, tag="kk_q", align_bytes=64)
+                kk_s = words.tile([P, H, MAIN], U8, tag="kk_s", align_bytes=64)
+                held["kk_q", g] = (kk_q, kk_s)
+            kk_bf = held["kk_bf", g][0]
+            kk_q, kk_s = held["kk_q", g]
+            for h in heads:
                 nc.vector.quantize_mx(
                     out=kk_q[:, h, :].bitcast(FP8X4),
                     scales=kk_s[:, h, :],
                     in_=kk_bf[:, h, :, :].rearrange("p c t -> p (c t)"),
                 )
-            nc.vector.quantize_mx(
-                out=tail_q[g % 3][:, 0:TAIL].bitcast(FP8X4),
-                scales=tail_s[g % 3][:, 0:TAIL],
-                in_=kk_tail[:].rearrange("p c t -> p (c t)"),
-            )
-            held["kk_q", g] = (kk_q, kk_s)
 
         def main_passes(g, heads):
             if g % GROUPS == 0 and 0 in heads:
@@ -510,67 +518,69 @@ def tile_taylorsoftmaxattention_pa_t_kernel(
         quantise_x(1)
         floor_norm(0)
         factors(0)
+        root(0)
         norm(0)
         project(1)
         turn_x(2, (0, 1, 2, 3))
         v_to_tokens(0)
         copy_kn(0)
-        quantise_x(2)
         sum_squares(1)
+        quantise_x(2)
+        floor_norm(1)
+        factors(1)
         for g in range(n_groups):
             last_of_batch = g % GROUPS == GROUPS - 1
             done = g // GROUPS - 1
             following = g + 1 < n_groups
-            if following:
-                k_to_tokens(g + 1)
-                floor_norm(g + 1)
             new_products(g)
-            large_blocks(g, (0, 1, 2))
+            large_blocks(g, (0, 1, 2, 3))
+            if g + X_AHEAD < n_groups:
+                load(g + X_AHEAD)
             if following:
-                factors(g + 1)
-            large_blocks(g, (3,))
-            diagonal(g)
+                root(g + 1)
             if g + 3 < n_groups:
                 turn_x(g + 3, (0, 1))
-            if g >= 1:
-                main_passes(g - 1, (0, 1))
+            diagonal(g)
+            if following:
+                k_to_tokens(g + 1)
             if g + 3 < n_groups:
-                turn_x(g + 3, (2,))
-            if g >= 1:
-                main_passes(g - 1, (2, 3))
-            if g + 3 < n_groups:
-                turn_x(g + 3, (3,))
+                turn_x(g + 3, (2, 3))
             small_blocks(g, (0, 1, 2, 3))
             if g + 2 < n_groups:
                 project(g + 2)
+            if g >= 1:
+                main_passes(g - 1, (0, 1, 2, 3))
             if following:
                 v_to_tokens(g + 1)
             if done >= 0 and not last_of_batch:
                 tail_and_kv(done)
             if last_of_batch:
                 float_sums(g // GROUPS)
+            if g + 2 < n_groups:
+                sum_squares(g + 2)
             if following:
                 norm(g + 1)
-            if g + 4 < n_groups:
-                load(g + 4)
-            if following:
                 copy_kn(g + 1)
-            if last_of_batch:
-                float_columns(g // GROUPS)
             strips(g)
+            quantise_v(g)
+            quantise_kn(g)
+            if g + 2 < n_groups:
+                floor_norm(g + 2)
+            quantise_tail(g)
+            mask_v(g)
+            quantise_products(g, (3,))
+            if g + 2 < n_groups:
+                factors(g + 2)
             if g + 3 < n_groups:
                 quantise_x(g + 3)
-            quantise_v(g)
-            quantise_products(g)
-            quantise_kn(g)
-            mask_v(g)
+            quantise_products(g, (0, 1, 2))
+            if last_of_batch:
+                float_columns(g // GROUPS)
             if done >= 0 and not last_of_batch:
                 spread_blocks(done)
                 spread_strips(done)
             if done >= 0 and last_of_batch:
                 kv_mod_out(done)
-            if g + 2 < n_groups:
-                sum_squares(g + 2)
         main_passes(n_groups - 1, (0, 1, 2, 3))
         tail_and_kv(B - 1)
         spread_blocks(B - 1)

@@ -31,6 +31,7 @@ TAIL_STRIP = 3
 STRIPS = (0, 1, 2, 4, 5, 6)
 STRIP_START = {0: 416, 1: 444, 2: 468, 4: 488, 5: 500, 6: 508}
 TAIL = H * N_BLK * (BLK - 1 - TAIL_STRIP)
+HEAD_ORDER = (3, 0, 1, 2)
 X_AHEAD = 6
 L_PITCH = N_BLK * (D + BLK)
 GPSIMD_HEADS = (0, 1, 2)
@@ -60,10 +61,11 @@ def tile_taylorsoftmaxattention_pa_t_kernel(
         def load(g):
             b, part = divmod(g, GROUPS)
             xs = x_pool.tile([P, PACK, C], BF16, tag="xs")
-            nc.sync.dma_start(
-                out=xs[:],
-                in_=x[b, K_PASS * part : K_PASS * (part + 1), :].rearrange("(p t) c -> p t c", t=PACK),
-            )
+            rows = x[b, K_PASS * part : K_PASS * (part + 1), :].rearrange("(p t) c -> p t c", t=PACK)
+            pieces = 2 if g == 0 else 1
+            for n in range(pieces):
+                tokens = slice(PACK // pieces * n, PACK // pieces * (n + 1))
+                nc.sync.dma_start(out=xs[:, tokens, :], in_=rows[:, tokens, :])
             held["xs", g] = xs
 
         load(0)
@@ -124,8 +126,12 @@ def tile_taylorsoftmaxattention_pa_t_kernel(
         for n in range(4):
             nc.scalar.copy(out=kn_tok[n][:, :, P : P + 1], in_=ones[:].unsqueeze(2))
         v_sums = const.tile([P, B * GROUPS], F32)
+        sums_sq = const.tile([P, P], F32)
+        nc.gpsimd.memset(sums_sq[:], 0.0)
+        vsum_tile = const.tile([P, H, D + 1], F32)
+        nc.gpsimd.memset(vsum_tile[0:D, :, 0:1], 1.0)
 
-        def turn_x(g, quarters):
+        def turn_x(g, quarters, by_vector=()):
             xs = held["xs", g]
             if 0 in quarters:
                 x_grouped = work.tile([P, C_PASSES * K_PASS * PACK], BF16, tag="x_grouped", align_bytes=64)
@@ -142,10 +148,11 @@ def tile_taylorsoftmaxattention_pa_t_kernel(
                             x_words[:, 256 * c + u : 256 * (c + 1) : 2],
                             ident[:],
                         )
-                nc.scalar.copy(
-                    out=grouped_words[:, c, 2 * P * half : 2 * P * (half + 1), :],
-                    in_=turned[:].rearrange("p u n -> p n u"),
-                )
+                out = grouped_words[:, c, 2 * P * half : 2 * P * (half + 1), :]
+                if quarter in by_vector:
+                    nc.vector.tensor_copy(out=out, in_=turned[:].rearrange("p u n -> p n u"))
+                else:
+                    nc.scalar.copy(out=out, in_=turned[:].rearrange("p u n -> p n u"))
 
         def quantise_x(g):
             x_q = work.tile([P, C_PASSES * K_PASS], U32, tag="x_q", align_bytes=64)
@@ -173,8 +180,8 @@ def tile_taylorsoftmaxattention_pa_t_kernel(
             kT = work.tile([P, K_PASS], F32, tag="kT")
             squares = work.tile([P, K_PASS], F32, tag="squares")
             vT = work.tile([P, K_PASS], F32, tag="vT")
-            nc.scalar.activation(out=kT[:], in_=sums[0][:], func=ACT.Identity, bias=bias_col[:, 0:1], scale=1.0)
             nc.scalar.activation(out=squares[:], in_=sums[0][:], func=ACT.Square, bias=bias_col[:, 0:1], scale=1.0)
+            nc.scalar.activation(out=kT[:], in_=sums[0][:], func=ACT.Identity, bias=bias_col[:, 0:1], scale=1.0)
             nc.scalar.activation(
                 out=vT[:],
                 in_=sums[1][:],
@@ -361,48 +368,49 @@ def tile_taylorsoftmaxattention_pa_t_kernel(
                     in_=kk_bf[:, h, :, :].rearrange("p c t -> p (c t)"),
                 )
 
-        def main_passes(g, heads):
-            if g % GROUPS == 0 and 0 in heads:
+        def main_passes(g):
+            if g % GROUPS == 0:
                 z_main = main_ps.tile([P, MAIN], F32, tag="z_main")
                 held["z_main", g // GROUPS] = z_main
             z_main = held["z_main", g // GROUPS]
             v_masked = v_mask[g % 3][:].rearrange("p h x -> p (h x)")
             v_s = held["v_q", g][1]
             kk_q, kk_s = held["kk_q", g]
-            for h in heads:
+            for h in HEAD_ORDER:
                 nc.tensor.matmul_mx(
                     out=z_main[:],
                     lhsT=v_masked[:, P * h : P * (h + 1)].bitcast(FP8X4),
                     lhsT_scale=v_s[:],
                     rhs=kk_q[:, h, :].bitcast(FP8X4),
                     rhs_scale=kk_s[:, h, :],
-                    start=(g % GROUPS == 0 and h == 0),
-                    stop=(g % GROUPS == GROUPS - 1 and h == H - 1),
+                    start=(g % GROUPS == 0 and h == HEAD_ORDER[0]),
+                    stop=(g % GROUPS == GROUPS - 1 and h == HEAD_ORDER[-1]),
                 )
 
-        def float_sums(b):
+        def float_sums(g):
+            b, part = divmod(g, GROUPS)
+            if part == 0:
+                mn = misc_ps.tile([P, P + 1], F32, tag="misc")
+                held["mn", b] = mn
+            mn, tok = held["mn", b], kn_tok[g % 4]
+            for t in range(PACK):
+                nc.tensor.matmul(
+                    out=mn[:],
+                    lhsT=tok[:, t, 0:P],
+                    rhs=tok[:, t, 0 : P + 1],
+                    start=(part == 0 and t == 0),
+                    stop=(part == GROUPS - 1 and t == PACK - 1),
+                )
+
+        def float_columns(b):
             o_tile = work.tile([P, H, BLK, D + 1], F32, tag="o_tile")
             kv_tile = work.tile([P, D + 1], F32, tag="kv_tile")
             held["o_tile", b] = o_tile
             held["kv_tile", b] = kv_tile
-            mn = misc_ps.tile([P, P + 1], F32, tag="misc")
-            for part in range(GROUPS):
-                tok = kn_tok[(GROUPS * b + part) % 4]
-                for t in range(PACK):
-                    nc.tensor.matmul(
-                        out=mn[:],
-                        lhsT=tok[:, t, 0:P],
-                        rhs=tok[:, t, 0 : P + 1],
-                        start=(part == 0 and t == 0),
-                        stop=(part == GROUPS - 1 and t == PACK - 1),
-                    )
+            mn = held["mn", b]
             mn_sb = work.tile([P, P + 1], F32, tag="mn_sb")
             nc.scalar.mul(out=mn_sb[:], in_=mn[:], mul=1.0 / N_TOK)
             nc.scalar.copy(out=kv_tile[:, 0:1], in_=mn_sb[:, P : P + 1])
-            held["mn_sb", b] = mn_sb
-
-        def float_columns(b):
-            mn_sb, o_tile = held["mn_sb", b], held["o_tile", b]
             q = misc_ps.tile([P, P], F32, tag="misc")
             for h in range(H):
                 own = slice(D * h, D * (h + 1))
@@ -415,7 +423,7 @@ def tile_taylorsoftmaxattention_pa_t_kernel(
                 )
 
         def tail_and_kv(b):
-            sums = misc_ps.tile([P, 2, P], F32, tag="misc", name="tail_and_kv_sums")
+            sums = turn_ps.tile([P, 2, P], F32, tag="turn", name="tail_and_kv_sums")
             for part in range(GROUPS):
                 g = GROUPS * b + part
                 v_q, v_s = held["v_q", g]
@@ -443,10 +451,11 @@ def tile_taylorsoftmaxattention_pa_t_kernel(
                 )
             tail_sb = work.tile([P, TAIL // H], F32, tag="tail_sb")
             kv_tile = held["kv_tile", b]
+            copy = nc.vector.tensor_copy if b == B - 1 else nc.scalar.copy
             for h in range(H):
                 own = slice(D * h, D * (h + 1))
-                nc.scalar.copy(out=tail_sb[own, :], in_=sums[own, 0, TAIL // H * h : TAIL // H * (h + 1)])
-                nc.scalar.copy(out=kv_tile[own, 1 : D + 1], in_=sums[own, 1, own])
+                copy(out=tail_sb[own, :], in_=sums[own, 0, TAIL // H * h : TAIL // H * (h + 1)])
+                copy(out=kv_tile[own, 1 : D + 1], in_=sums[own, 1, own])
             nc.sync.dma_start(out=out_1[b].rearrange("h d c -> (h d) c"), in_=kv_tile[:])
             held["tail_sb", b] = tail_sb
 
@@ -492,7 +501,8 @@ def tile_taylorsoftmaxattention_pa_t_kernel(
                     nc.tensor.transpose(
                         turned[:, n, :], z_sq[:, PACK * half + n, 0:P], ident[:]
                     )
-                nc.scalar.copy(
+                copy = nc.vector.tensor_copy if b == B - 1 and half == 1 else nc.scalar.copy
+                copy(
                     out=o_tile[:, :, PACK * half : PACK * (half + 1), 1 : D + 1],
                     in_=turned[:].rearrange("p l (h e) -> p h l e", h=H),
                 )
@@ -502,7 +512,25 @@ def tile_taylorsoftmaxattention_pa_t_kernel(
                     in_=o_tile[D * J : D * (J + 1)].rearrange("p h l c -> p h (l c)"),
                 )
 
-        turn_x(0, (0, 1, 2, 3))
+        def vsum_out():
+            nc.vector.tensor_tensor(
+                out=sums_sq[:, 0:B], in0=v_sums[:, 0 : B * GROUPS : 2], in1=v_sums[:, 1 : B * GROUPS : 2], op=ALU.add
+            )
+            sums_ps = turn_ps.tile([P, P], F32, tag="turn", name="sums_ps")
+            nc.tensor.transpose(sums_ps[:], sums_sq[:], ident[:])
+            nc.scalar.copy(
+                out=vsum_tile[0:D, :, 1 : D + 1], in_=sums_ps[0:D, :].rearrange("p (h e) -> p h e", h=H)
+            )
+            nc.sync.dma_start(
+                out=out_2.rearrange("b h o c -> b (h o c)"), in_=vsum_tile[0:B].rearrange("p h c -> p (h c)")
+            )
+
+        def first_products(g):
+            new_products(g)
+            large_blocks(g, (0, 1, 2, 3))
+            small_blocks(g, (0, 1, 2, 3))
+
+        turn_x(0, (0, 2, 1, 3), (2, 3))
         bias_rows_f = const.tile([P, P], F32)
         nc.vector.tensor_copy(out=bias_rows_f[:], in_=bias_rows[:])
         bias_ps = turn_ps.tile([P, P], F32, tag="turn")
@@ -511,29 +539,28 @@ def tile_taylorsoftmaxattention_pa_t_kernel(
         nc.scalar.copy(out=bias_col[:, 0:1], in_=bias_ps[:, 0:1])
         nc.scalar.mul(out=bias_col[:, 1:2], in_=bias_ps[:, 1:2], mul=1.0 / N_TOK)
         quantise_x(0)
-        turn_x(1, (0, 1, 2, 3))
+        turn_x(1, (0, 1, 2, 3), (1, 3))
         project(0)
+        quantise_x(1)
         sum_squares(0)
         k_to_tokens(0)
-        quantise_x(1)
         floor_norm(0)
         factors(0)
         root(0)
         norm(0)
         project(1)
-        turn_x(2, (0, 1, 2, 3))
+        first_products(0)
         v_to_tokens(0)
         copy_kn(0)
+        turn_x(2, (0, 1, 2, 3))
         sum_squares(1)
-        quantise_x(2)
         floor_norm(1)
         factors(1)
+        quantise_x(2)
         for g in range(n_groups):
             last_of_batch = g % GROUPS == GROUPS - 1
             done = g // GROUPS - 1
             following = g + 1 < n_groups
-            new_products(g)
-            large_blocks(g, (0, 1, 2, 3))
             if g + X_AHEAD < n_groups:
                 load(g + X_AHEAD)
             if following:
@@ -545,19 +572,21 @@ def tile_taylorsoftmaxattention_pa_t_kernel(
                 k_to_tokens(g + 1)
             if g + 3 < n_groups:
                 turn_x(g + 3, (2, 3))
-            small_blocks(g, (0, 1, 2, 3))
             if g + 2 < n_groups:
                 project(g + 2)
-            if g >= 1:
-                main_passes(g - 1, (0, 1, 2, 3))
+            if g >= 1 and not last_of_batch:
+                main_passes(g - 1)
             if following:
                 v_to_tokens(g + 1)
             if done >= 0 and not last_of_batch:
                 tail_and_kv(done)
-            if last_of_batch:
-                float_sums(g // GROUPS)
+            if done >= 0 and last_of_batch:
+                kv_mod_out(done)
             if g + 2 < n_groups:
                 sum_squares(g + 2)
+            float_sums(g)
+            if last_of_batch:
+                main_passes(g - 1)
             if following:
                 norm(g + 1)
                 copy_kn(g + 1)
@@ -568,37 +597,23 @@ def tile_taylorsoftmaxattention_pa_t_kernel(
                 floor_norm(g + 2)
             quantise_tail(g)
             mask_v(g)
-            quantise_products(g, (3,))
+            quantise_products(g, HEAD_ORDER[:1])
             if g + 2 < n_groups:
                 factors(g + 2)
             if g + 3 < n_groups:
                 quantise_x(g + 3)
-            quantise_products(g, (0, 1, 2))
+            quantise_products(g, HEAD_ORDER[1:])
+            if g == n_groups - 2:
+                vsum_out()
+            if following:
+                first_products(g + 1)
             if last_of_batch:
                 float_columns(g // GROUPS)
             if done >= 0 and not last_of_batch:
                 spread_blocks(done)
                 spread_strips(done)
-            if done >= 0 and last_of_batch:
-                kv_mod_out(done)
-        main_passes(n_groups - 1, (0, 1, 2, 3))
+        main_passes(n_groups - 1)
         tail_and_kv(B - 1)
         spread_blocks(B - 1)
         spread_strips(B - 1)
         kv_mod_out(B - 1)
-
-        sums_sq = const.tile([P, P], F32)
-        nc.vector.memset(sums_sq[:], 0.0)
-        nc.vector.tensor_tensor(
-            out=sums_sq[:, 0:B], in0=v_sums[:, 0 : B * GROUPS : 2], in1=v_sums[:, 1 : B * GROUPS : 2], op=ALU.add
-        )
-        sums_ps = turn_ps.tile([P, P], F32, tag="turn")
-        nc.tensor.transpose(sums_ps[:], sums_sq[:], ident[:])
-        vsum_tile = const.tile([P, H, D + 1], F32)
-        nc.vector.memset(vsum_tile[0:D, :, 0:1], 1.0)
-        nc.vector.tensor_copy(
-            out=vsum_tile[0:D, :, 1 : D + 1], in_=sums_ps[0:D, :].rearrange("p (h e) -> p h e", h=H)
-        )
-        nc.scalar.dma_start(
-            out=out_2.rearrange("b h o c -> b (h o c)"), in_=vsum_tile[0:B].rearrange("p h c -> p (h c)")
-        )

@@ -34,7 +34,8 @@ TAIL = H * N_BLK * (BLK - 1 - TAIL_STRIP)
 HEAD_ORDER = (3, 0, 1, 2)
 X_AHEAD = 6
 L_PITCH = N_BLK * (D + BLK)
-GPSIMD_HEADS = (0, 1, 2)
+GPSIMD_ROWS = (16, 16, 12)
+VECTOR_ROWS = ((3, 0), (3, BLK), (2, 12))
 
 FLOPS = 2 * B * N_TOK * C * 2 * H * D + 2 * B * H * N_TOK * D * D * D + 2 * B * H * N_TOK * D * D
 
@@ -88,9 +89,21 @@ def tile_taylorsoftmaxattention_pa_t_kernel(
                     in_=scales[:, 4 * quad : 4 * quad + 4, :].rearrange("c r n -> r c n").bitcast(I32),
                 )
 
+        k_words = const.tile([P, C_PASSES, P], I32, align_bytes=64)
+        k_scales = const.tile([P, C_PASSES, P], U8, align_bytes=64)
+        for to, given in ((k_words, w_words[:, 0:C_PASSES, :].bitcast(I32)), (k_scales, w_scales[:, 0:C_PASSES, :])):
+            for half in range(2):
+                nc.gpsimd.tensor_copy(
+                    out=to[:, :, P // 2 * half : P // 2 * (half + 1)].rearrange("p c (m a) -> p c m a", a=BLK),
+                    in_=given.rearrange("p c (m s a) -> p c m s a", s=2, a=BLK)[:, :, :, half, :],
+                )
+
         bias_rows = const.tile([P, P], BF16)
         nc.vector.memset(bias_rows[:], 0.0)
-        nc.sync.dma_start(out=bias_rows[0:1, :], in_=bk.unsqueeze(0))
+        nc.sync.dma_start(
+            out=bias_rows[0:1, :].rearrange("p (s m a) -> p s m a", s=2, a=BLK),
+            in_=bk.rearrange("(m s a) -> s m a", s=2, a=BLK).unsqueeze(0),
+        )
         nc.sync.dma_start(out=bias_rows[1:2, :], in_=bv.unsqueeze(0))
         load(1)
         load(2)
@@ -109,7 +122,7 @@ def tile_taylorsoftmaxattention_pa_t_kernel(
             nc.vector.tensor_copy(out=rep_head[own, h, :], in_=rep[own].rearrange("k J i -> k (J i)"))
         of_head = const.tile([P, H], F32)
         nc.vector.tensor_reduce(
-            out=of_head[:], in_=ident[:].rearrange("k (h d) -> k h d", h=H), axis=AX.X, op=ALU.add
+            out=of_head[:], in_=ident[:].rearrange("k (s h x) -> k h s x", s=2, h=H), axis=AX.XY, op=ALU.add
         )
         ones = const.tile([P, PACK], F32)
         nc.vector.memset(ones[:], 1.0)
@@ -163,14 +176,15 @@ def tile_taylorsoftmaxattention_pa_t_kernel(
         def project(g):
             x_q, x_s = held["x_q", g]
             sums = []
-            for w in range(2):
+            given = (k_words[:].bitcast(U32), k_scales[:]), (w_words[:, C_PASSES:], w_scales[:, C_PASSES:])
+            for words_of, scales_of in given:
                 acc = turn_ps.tile([P, K_PASS], F32, tag="turn", name="acc")
                 for c in range(C_PASSES):
                     cols = slice(K_PASS * c, K_PASS * (c + 1))
                     nc.tensor.matmul_mx(
                         out=acc[:],
-                        lhsT=w_words[:, C_PASSES * w + c, :].bitcast(FP8X4),
-                        lhsT_scale=w_scales[:, C_PASSES * w + c, :],
+                        lhsT=words_of[:, c, :].bitcast(FP8X4),
+                        lhsT_scale=scales_of[:, c, :],
                         rhs=x_q[:, cols].bitcast(FP8X4),
                         rhs_scale=x_s[:, cols],
                         start=(c == 0),
@@ -238,24 +252,31 @@ def tile_taylorsoftmaxattention_pa_t_kernel(
             held["r2", g] = r2
 
         def root(g):
-            r1 = work.tile([P, PACK * H], F32, tag="r1")
-            nc.scalar.activation(out=r1[:], in_=held["r2", g][:], func=ACT.Sqrt)
-            held["r1", g] = r1
-
-        def scale_k(g, factor, tag):
-            scaled = work.tile([P, P, PACK], F32, tag=tag, name=tag)
-            nc.vector.tensor_tensor(
-                out=scaled[:].rearrange("p (h d) t -> p h d t", h=H),
-                in0=held["k_tok", g][:].rearrange("p t (h d) -> p h d t", h=H),
-                in1=factor[:].rearrange("p (t h) -> p h t", h=H).unsqueeze(2).to_broadcast([P, H, D, PACK]),
-                op=ALU.mult,
-            )
-            return scaled
+            by_group = held["r2", g][:].unsqueeze(2).to_broadcast([P, PACK * H, 2])
+            r1 = work.tile([P, PACK * H, 2], F32, tag="r1")
+            nc.scalar.activation(out=r1[:], in_=by_group, func=ACT.Sqrt)
+            r2 = work.tile([P, PACK * H, 2], F32, tag="r2_by_group")
+            nc.scalar.copy(out=r2[:], in_=by_group)
+            held["factors", g] = (r1, r2)
 
         def norm(g):
-            kn = scale_k(g, held["r1", g], "kn")
-            held["kn", g] = kn
-            held["k_r2", g] = scale_k(g, held["r2", g], "k_r2")
+            r1, r2 = held["factors", g]
+            for name, factor in (("kn", r1), ("k_r2", r2)):
+                scaled = work.tile([P, P, PACK], F32, tag=name, name=name)
+                by_half = scaled[:].rearrange("p (m s a) t -> p s m a t", s=2, a=BLK)
+                for half in range(2):
+                    nc.vector.tensor_tensor(
+                        out=by_half[:, half],
+                        in0=held["k_tok", g][:, :, P // 2 * half : P // 2 * (half + 1)].rearrange(
+                            "p t (m a) -> p m a t", a=BLK
+                        ),
+                        in1=factor[:]
+                        .rearrange("p (t h) b -> p (h b) t", h=H)
+                        .unsqueeze(2)
+                        .to_broadcast([P, 2 * H, BLK, PACK]),
+                        op=ALU.mult,
+                    )
+                held[name, g] = scaled
 
         def copy_kn(g):
             kn = held["kn", g]
@@ -288,36 +309,51 @@ def tile_taylorsoftmaxattention_pa_t_kernel(
             kk_tail = single.tile([P, TAIL, PACK], BF16, tag="kk_tail", align_bytes=64)
             held["kk_bf", g] = (kk_bf, kk_tail)
 
-        def square_block(g, h, start, i, j, side):
+        def large_blocks(g):
             k_tok, k_r2, kn = held["k_tok", g], held["k_r2", g], held["kn", g]
             kk_bf = held["kk_bf", g][0]
-            shape = [P, side, side, PACK]
-            out = kk_bf[:, h, start : start + side * side, :].rearrange("p (i j) t -> p i j t", i=side)
-            rows = slice(D * h + i, D * h + i + side)
-            cols = slice(D * h + j, D * h + j + side)
-            if side == HALF and h in GPSIMD_HEADS:
+            for h, rows in enumerate(GPSIMD_ROWS):
+                shape = [P, rows, HALF, PACK]
                 nc.gpsimd.tensor_tensor(
-                    out=out,
-                    in0=kn[:, rows, :].unsqueeze(2).to_broadcast(shape),
-                    in1=kn[:, cols, :].unsqueeze(1).to_broadcast(shape),
+                    out=kk_bf[:, h, 0 : HALF * rows, :].rearrange("p (i j) t -> p i j t", j=HALF),
+                    in0=kn[:, D * h : D * h + rows, :].unsqueeze(2).to_broadcast(shape),
+                    in1=kn[:, D * h + HALF : D * (h + 1), :].unsqueeze(1).to_broadcast(shape),
                     op=ALU.mult,
                 )
-            else:
+            for h, first_row in VECTOR_ROWS:
+                half, a_first = divmod(first_row, BLK)
+                rows = BLK - a_first
+                i_first = P // 2 * half + 2 * BLK * h + a_first
+                shape = [P, rows, HALF, PACK]
                 nc.vector.tensor_tensor(
-                    out=out,
-                    in0=k_tok[:].rearrange("p t f -> p f t")[:, rows, :].unsqueeze(2).to_broadcast(shape),
-                    in1=k_r2[:, cols, :].unsqueeze(1).to_broadcast(shape),
+                    out=kk_bf[:, h, HALF * first_row : HALF * (first_row + rows), :].rearrange(
+                        "p (i j) t -> p i j t", i=rows
+                    ),
+                    in0=k_tok[:, :, i_first : i_first + rows]
+                    .rearrange("p t i -> p i t")
+                    .unsqueeze(2)
+                    .to_broadcast(shape),
+                    in1=k_r2[:, D * h + HALF : D * (h + 1), :].unsqueeze(1).to_broadcast(shape),
                     op=ALU.mult,
                 )
 
-        def large_blocks(g, heads):
-            for h in heads:
-                square_block(g, h, 0, 0, HALF, HALF)
-
-        def small_blocks(g, heads):
-            for h in heads:
-                for b in range(2):
-                    square_block(g, h, MID_START + BLK * BLK * b, HALF * b, HALF * b + BLK, BLK)
+        def small_blocks(g):
+            k_tok, k_r2 = held["k_tok", g], held["k_r2", g]
+            shape = [P, H, 2, BLK, BLK, PACK]
+            nc.vector.tensor_tensor(
+                out=held["kk_bf", g][0][:, :, MID_START:DIAG_START, :].rearrange(
+                    "p h (b a c) t -> p h b a c t", b=2, a=BLK
+                ),
+                in0=k_tok[:, :, 0 : P // 2]
+                .rearrange("p t (h b a) -> p h b a t", h=H, b=2)
+                .unsqueeze(4)
+                .to_broadcast(shape),
+                in1=k_r2[:]
+                .rearrange("p (h b s c) t -> p s h b c t", h=H, b=2, s=2)[:, 1]
+                .unsqueeze(3)
+                .to_broadcast(shape),
+                op=ALU.mult,
+            )
 
         def diagonal(g):
             kk_bf, kn = held["kk_bf", g][0], held["kn", g]
@@ -328,22 +364,19 @@ def tile_taylorsoftmaxattention_pa_t_kernel(
             )
 
         def strips(g):
-            k_rows = held["k_tok", g][:].rearrange("p t (h G a) -> p h G a t", h=H, G=N_BLK)
-            k_cols = held["k_r2", g][:].rearrange("p (h G a) t -> p h G a t", h=H, G=N_BLK)
+            k_rows = held["k_tok", g][:].rearrange("p t (s h b a) -> p s h b a t", s=2, h=H, b=2)
+            k_cols = held["k_r2", g][:].rearrange("p (h b s a) t -> p s h b a t", s=2, h=H, b=2)
             kk_bf, kk_tail = held["kk_bf", g]
             for a in range(BLK - 1):
                 width = BLK - 1 - a
-                shape = [P, H, N_BLK, width, PACK]
                 if a == TAIL_STRIP:
-                    out = kk_tail[:].rearrange("p (h G w) t -> p h G w t", h=H, G=N_BLK)
+                    out = kk_tail[:].rearrange("p (h x) t -> p h x t", h=H)
                 else:
-                    out = kk_bf[:, :, STRIP_START[a] : STRIP_START[a] + N_BLK * width, :].rearrange(
-                        "p h (G w) t -> p h G w t", G=N_BLK
-                    )
+                    out = kk_bf[:, :, STRIP_START[a] : STRIP_START[a] + N_BLK * width, :]
                 nc.vector.tensor_tensor(
-                    out=out,
-                    in0=k_rows[:, :, :, a : a + 1, :].to_broadcast(shape),
-                    in1=k_cols[:, :, :, a + 1 : BLK, :],
+                    out=out.rearrange("p h (s b w) t -> p s h b w t", s=2, b=2),
+                    in0=k_rows[:, :, :, :, a : a + 1, :].to_broadcast([P, 2, H, 2, width, PACK]),
+                    in1=k_cols[:, :, :, :, a + 1 : BLK, :],
                     op=ALU.mult,
                 )
 
@@ -465,6 +498,11 @@ def tile_taylorsoftmaxattention_pa_t_kernel(
             rows = z_sq[:, 0 : BLK * L_PITCH].rearrange("p (l x) -> p l x", l=BLK)
             square = rows[:, :, 0:P].rearrange("p l (J i) -> p l J i", J=N_BLK)
             middle = rows.rearrange("p l (b x) -> p l b x", b=2)
+            strip_results = z_main
+            if b == B - 1:
+                strip_results = work.tile([P, MAIN], F32, tag="strip_results")
+                nc.vector.tensor_copy(out=strip_results[:, DIAG_START:MAIN], in_=z_main[:, DIAG_START:MAIN])
+            held["strip_results", b] = strip_results
             z = z_main[:, 0:MID_START]
             nc.scalar.copy(out=square[:, :, 2:4, 0:HALF], in_=z.rearrange("p (i J l) -> p l J i", J=2, l=BLK))
             nc.scalar.copy(out=square[:, :, 0:2, HALF:D], in_=z.rearrange("p (J l j) -> p l J j", J=2, l=BLK))
@@ -475,23 +513,26 @@ def tile_taylorsoftmaxattention_pa_t_kernel(
             nc.scalar.copy(
                 out=middle[:, :, :, BLK : 2 * BLK], in_=z.rearrange("p (b l c) -> p l b c", b=2, l=BLK)
             )
-            nc.scalar.copy(
+            held["z_sq", b] = z_sq
+
+        def spread_strips(b):
+            z_sq, results, tail_sb = held["z_sq", b], held["strip_results", b], held["tail_sb", b]
+            diagonal = z_sq[:, 0 : BLK * L_PITCH].rearrange("p (l G x) -> p l G x", l=BLK, G=N_BLK)
+            copy = nc.vector.tensor_copy if b == B - 1 else nc.scalar.copy
+            copy(
                 out=z_sq[:].rearrange("p (a x) -> p a x", a=BLK)[:, :, 0:L_PITCH].rearrange(
                     "p a (G x) -> p a G x", G=N_BLK
                 )[:, :, :, 0],
-                in_=z_main[:, DIAG_START : DIAG_START + D].rearrange("p (G a) -> p a G", G=N_BLK),
+                in_=results[:, DIAG_START : DIAG_START + D].rearrange("p (G a) -> p a G", G=N_BLK),
             )
-            held["z_sq", b] = rows
-
-        def spread_strips(b):
-            z_main, tail_sb = held["z_main", b], held["tail_sb", b]
-            diagonal = held["z_sq", b].rearrange("p l (G x) -> p l G x", G=N_BLK)
             for a in range(BLK - 1):
                 width = BLK - 1 - a
-                z = tail_sb[:] if a == TAIL_STRIP else z_main[:, STRIP_START[a] : STRIP_START[a] + N_BLK * width]
-                z = z.rearrange("p (G w) -> p G w", G=N_BLK)
-                nc.scalar.copy(out=diagonal[:, a + 1 : BLK, :, a].rearrange("p w G -> p G w"), in_=z)
-                nc.scalar.copy(out=diagonal[:, a, :, a + 1 : BLK], in_=z)
+                z = tail_sb[:] if a == TAIL_STRIP else results[:, STRIP_START[a] : STRIP_START[a] + N_BLK * width]
+                z = z.rearrange("p (s b w) -> p s b w", s=2, b=2)
+                copy(
+                    out=diagonal[:, a + 1 : BLK, :, a].rearrange("p w (b s) -> p s b w", s=2), in_=z
+                )
+                copy(out=diagonal[:, a, :, a + 1 : BLK].rearrange("p (b s) w -> p s b w", s=2), in_=z)
 
         def kv_mod_out(b):
             o_tile, z_sq = held["o_tile", b], held["z_sq", b]
@@ -499,7 +540,7 @@ def tile_taylorsoftmaxattention_pa_t_kernel(
                 turned = turn_ps.tile([P, PACK, P], F32, tag="turn")
                 for n in range(PACK):
                     nc.tensor.transpose(
-                        turned[:, n, :], z_sq[:, PACK * half + n, 0:P], ident[:]
+                        turned[:, n, :], z_sq[:, L_PITCH * (PACK * half + n) : L_PITCH * (PACK * half + n) + P], ident[:]
                     )
                 copy = nc.vector.tensor_copy if b == B - 1 and half == 1 else nc.scalar.copy
                 copy(
@@ -527,8 +568,8 @@ def tile_taylorsoftmaxattention_pa_t_kernel(
 
         def first_products(g):
             new_products(g)
-            large_blocks(g, (0, 1, 2, 3))
-            small_blocks(g, (0, 1, 2, 3))
+            large_blocks(g)
+            small_blocks(g)
 
         turn_x(0, (0, 2, 1, 3), (2, 3))
         bias_rows_f = const.tile([P, P], F32)

@@ -34,8 +34,8 @@ TAIL = H * N_BLK * (BLK - 1 - TAIL_STRIP)
 HEAD_ORDER = (3, 0, 1, 2)
 X_AHEAD = 6
 L_PITCH = N_BLK * (D + BLK)
-GPSIMD_ROWS = (16, 16, 12)
-VECTOR_ROWS = ((3, 0), (3, BLK), (2, 12))
+GPSIMD_HEADS = (0, 1, 2)
+VECTOR_ROWS = ((3, 0), (3, BLK))
 
 FLOPS = 2 * B * N_TOK * C * 2 * H * D + 2 * B * H * N_TOK * D * D * D + 2 * B * H * N_TOK * D * D
 
@@ -294,9 +294,8 @@ def tile_taylorsoftmaxattention_pa_t_kernel(
             held["v_q", g] = (v_q, v_s)
 
         def mask_v(g):
-            nc.vector.tensor_copy(
-                out=v_mask[g % 3][:, :, 0:D], in_=held["v_q", g][0][:].rearrange("p (h e) -> p h e", h=H)
-            )
+            move = nc.vector.tensor_copy if g == n_groups - 1 else nc.scalar.dma_start
+            move(out=v_mask[g % 3][:, :, 0:D], in_=held["v_q", g][0][:].rearrange("p (h e) -> p h e", h=H))
 
         def quantise_kn(g):
             kn_q = words.tile([P, P], U32, tag="kn_q", align_bytes=64)
@@ -312,11 +311,11 @@ def tile_taylorsoftmaxattention_pa_t_kernel(
         def large_blocks(g):
             k_tok, k_r2, kn = held["k_tok", g], held["k_r2", g], held["kn", g]
             kk_bf = held["kk_bf", g][0]
-            for h, rows in enumerate(GPSIMD_ROWS):
-                shape = [P, rows, HALF, PACK]
+            for h in GPSIMD_HEADS:
+                shape = [P, HALF, HALF, PACK]
                 nc.gpsimd.tensor_tensor(
-                    out=kk_bf[:, h, 0 : HALF * rows, :].rearrange("p (i j) t -> p i j t", j=HALF),
-                    in0=kn[:, D * h : D * h + rows, :].unsqueeze(2).to_broadcast(shape),
+                    out=kk_bf[:, h, 0:MID_START, :].rearrange("p (i j) t -> p i j t", i=HALF),
+                    in0=kn[:, D * h : D * h + HALF, :].unsqueeze(2).to_broadcast(shape),
                     in1=kn[:, D * h + HALF : D * (h + 1), :].unsqueeze(1).to_broadcast(shape),
                     op=ALU.mult,
                 )
@@ -606,6 +605,8 @@ def tile_taylorsoftmaxattention_pa_t_kernel(
                 load(g + X_AHEAD)
             if following:
                 root(g + 1)
+            if g >= 1:
+                mask_v(g - 1)
             if g + 3 < n_groups:
                 turn_x(g + 3, (0, 1))
             diagonal(g)
@@ -637,7 +638,8 @@ def tile_taylorsoftmaxattention_pa_t_kernel(
             if g + 2 < n_groups:
                 floor_norm(g + 2)
             quantise_tail(g)
-            mask_v(g)
+            if not following:
+                mask_v(g)
             quantise_products(g, HEAD_ORDER[:1])
             if g + 2 < n_groups:
                 factors(g + 2)

@@ -31,10 +31,9 @@ TAIL_STRIP = 3
 STRIPS = (0, 1, 2, 4, 5, 6)
 STRIP_START = {0: 416, 1: 444, 2: 468, 4: 488, 5: 500, 6: 508}
 TAIL = H * N_BLK * (BLK - 1 - TAIL_STRIP)
-HEAD_ORDER = (3, 0, 1, 2)
 X_AHEAD = 6
 L_PITCH = N_BLK * (D + BLK)
-GPSIMD_HEADS = (0, 1, 2)
+GPSIMD_HEADS = 3
 VECTOR_ROWS = ((3, 0), (3, BLK))
 
 FLOPS = 2 * B * N_TOK * C * 2 * H * D + 2 * B * H * N_TOK * D * D * D + 2 * B * H * N_TOK * D * D
@@ -230,9 +229,9 @@ def tile_taylorsoftmaxattention_pa_t_kernel(
             v_tok = turn_ps.tile([P, PACK, P], F32, tag="turn", name="v_tok")
             for t in range(PACK):
                 nc.tensor.transpose(v_tok[:, t, :], held["vT", g][:, P * t : P * (t + 1)], ident[:])
-            v_bf = work.tile([P, P, PACK], BF16, tag="v_bf", align_bytes=64)
-            nc.scalar.copy(out=v_bf[:], in_=v_tok[:].rearrange("p t f -> p f t"))
-            held["v_bf", g] = v_bf
+            v_kn_bf = work.tile([P, 2, P, PACK], BF16, tag="v_kn_bf", align_bytes=64)
+            nc.scalar.copy(out=v_kn_bf[:, 0], in_=v_tok[:].rearrange("p t f -> p f t"))
+            held["v_kn_bf", g] = v_kn_bf
 
         def floor_norm(g):
             floored = work.tile([P, PACK * H], F32, tag="floored")
@@ -260,48 +259,48 @@ def tile_taylorsoftmaxattention_pa_t_kernel(
             held["factors", g] = (r1, r2)
 
         def norm(g):
-            r1, r2 = held["factors", g]
-            for name, factor in (("kn", r1), ("k_r2", r2)):
+            for name, order, factor in zip(
+                ("kn", "k_r2"), ("p (b h s a) t -> p s h b a t", "p (h b s a) t -> p s h b a t"), held["factors", g]
+            ):
                 scaled = work.tile([P, P, PACK], F32, tag=name, name=name)
-                by_half = scaled[:].rearrange("p (m s a) t -> p s m a t", s=2, a=BLK)
+                by_half = scaled[:].rearrange(order, h=H, b=2, s=2)
                 for half in range(2):
                     nc.vector.tensor_tensor(
                         out=by_half[:, half],
                         in0=held["k_tok", g][:, :, P // 2 * half : P // 2 * (half + 1)].rearrange(
-                            "p t (m a) -> p m a t", a=BLK
+                            "p t (h b a) -> p h b a t", h=H, b=2
                         ),
                         in1=factor[:]
-                        .rearrange("p (t h) b -> p (h b) t", h=H)
-                        .unsqueeze(2)
-                        .to_broadcast([P, 2 * H, BLK, PACK]),
+                        .rearrange("p (t h) b -> p h b t", h=H)
+                        .unsqueeze(3)
+                        .to_broadcast([P, H, 2, BLK, PACK]),
                         op=ALU.mult,
                     )
                 held[name, g] = scaled
 
         def copy_kn(g):
-            kn = held["kn", g]
-            nc.scalar.copy(out=kn_tok[g % 4][:, :, 0:P].rearrange("p t f -> p f t"), in_=kn[:])
-            kn_bf = work.tile([P, P * PACK], BF16, tag="kn_bf", align_bytes=64)
-            nc.scalar.copy(out=kn_bf[:], in_=kn[:].rearrange("p f t -> p (f t)"))
-            held["kn_bf", g] = kn_bf
-
-        def quantise_v(g):
-            v_q = words.tile([P, P], I32, tag="v_q", align_bytes=64)
-            v_s = words.tile([P, P], U8, tag="v_s", align_bytes=64)
-            nc.vector.quantize_mx(
-                out=v_q[:].bitcast(FP8X4), scales=v_s[:], in_=held["v_bf", g][:].rearrange("p f t -> p (f t)")
+            kn = held["kn", g][:].rearrange("p (b h x) t -> p b h x t", b=2, h=H)
+            tok = kn_tok[g % 4][:, :, 0:P].rearrange("p t (h b x) -> p b h x t", b=2, h=H)
+            for half in range(2):
+                nc.scalar.copy(out=tok[:, half], in_=kn[:, half])
+            nc.scalar.copy(
+                out=held["v_kn_bf", g][:, 1].rearrange("p (h b x) t -> p b h x t", b=2, h=H), in_=kn
             )
-            held["v_q", g] = (v_q, v_s)
+
+        def quantise_v_kn(g):
+            v_kn_q = words.tile([P, 2, P], I32, tag="v_kn_q", align_bytes=64)
+            v_kn_s = words.tile([P, 2, P], U8, tag="v_kn_s", align_bytes=64)
+            nc.vector.quantize_mx(
+                out=v_kn_q[:].rearrange("p n f -> p (n f)").bitcast(FP8X4),
+                scales=v_kn_s[:].rearrange("p n f -> p (n f)"),
+                in_=held["v_kn_bf", g][:].rearrange("p n f t -> p (n f t)"),
+            )
+            held["v_q", g] = (v_kn_q[:, 0, :], v_kn_s[:, 0, :])
+            held["kn_q", g] = (v_kn_q[:, 1, :], v_kn_s[:, 1, :])
 
         def mask_v(g):
             move = nc.vector.tensor_copy if g == n_groups - 1 else nc.scalar.dma_start
-            move(out=v_mask[g % 3][:, :, 0:D], in_=held["v_q", g][0][:].rearrange("p (h e) -> p h e", h=H))
-
-        def quantise_kn(g):
-            kn_q = words.tile([P, P], U32, tag="kn_q", align_bytes=64)
-            kn_s = words.tile([P, P], U8, tag="kn_s", align_bytes=64)
-            nc.vector.quantize_mx(out=kn_q[:].bitcast(FP8X4), scales=kn_s[:], in_=held["kn_bf", g][:])
-            held["kn_q", g] = (kn_q, kn_s)
+            move(out=v_mask[g % 3][:, :, 0:D], in_=held["v_q", g][0].rearrange("p (h e) -> p h e", h=H))
 
         def new_products(g):
             kk_bf = single.tile([P, H, MAIN, PACK], BF16, tag="kk_bf", align_bytes=64)
@@ -311,14 +310,14 @@ def tile_taylorsoftmaxattention_pa_t_kernel(
         def large_blocks(g):
             k_tok, k_r2, kn = held["k_tok", g], held["k_r2", g], held["kn", g]
             kk_bf = held["kk_bf", g][0]
-            for h in GPSIMD_HEADS:
-                shape = [P, HALF, HALF, PACK]
-                nc.gpsimd.tensor_tensor(
-                    out=kk_bf[:, h, 0:MID_START, :].rearrange("p (i j) t -> p i j t", i=HALF),
-                    in0=kn[:, D * h : D * h + HALF, :].unsqueeze(2).to_broadcast(shape),
-                    in1=kn[:, D * h + HALF : D * (h + 1), :].unsqueeze(1).to_broadcast(shape),
-                    op=ALU.mult,
-                )
+            shape = [P, GPSIMD_HEADS, HALF, HALF, PACK]
+            kn_halves = kn[:].rearrange("p (b h i) t -> p b h i t", b=2, h=H)
+            nc.gpsimd.tensor_tensor(
+                out=kk_bf[:, 0:GPSIMD_HEADS, 0:MID_START, :].rearrange("p h (i j) t -> p h i j t", i=HALF),
+                in0=kn_halves[:, 0, 0:GPSIMD_HEADS].unsqueeze(3).to_broadcast(shape),
+                in1=kn_halves[:, 1, 0:GPSIMD_HEADS].unsqueeze(2).to_broadcast(shape),
+                op=ALU.mult,
+            )
             for h, first_row in VECTOR_ROWS:
                 half, a_first = divmod(first_row, BLK)
                 rows = BLK - a_first
@@ -357,8 +356,8 @@ def tile_taylorsoftmaxattention_pa_t_kernel(
         def diagonal(g):
             kk_bf, kn = held["kk_bf", g][0], held["kn", g]
             nc.scalar.activation(
-                out=kk_bf[:, :, DIAG_START : DIAG_START + D, :],
-                in_=kn[:].rearrange("p (h f) t -> p h f t", h=H),
+                out=kk_bf[:, :, DIAG_START : DIAG_START + D, :].rearrange("p h (b x) t -> p h b x t", b=2),
+                in_=kn[:].rearrange("p (b h x) t -> p h b x t", b=2, h=H),
                 func=ACT.Square,
             )
 
@@ -386,19 +385,19 @@ def tile_taylorsoftmaxattention_pa_t_kernel(
                 in_=held["kk_bf", g][1][:].rearrange("p c t -> p (c t)"),
             )
 
-        def quantise_products(g, heads):
+        def quantise_products(g, pair):
             if ("kk_q", g) not in held:
                 kk_q = words.tile([P, H, MAIN], U32, tag="kk_q", align_bytes=64)
                 kk_s = words.tile([P, H, MAIN], U8, tag="kk_s", align_bytes=64)
                 held["kk_q", g] = (kk_q, kk_s)
             kk_bf = held["kk_bf", g][0]
             kk_q, kk_s = held["kk_q", g]
-            for h in heads:
-                nc.vector.quantize_mx(
-                    out=kk_q[:, h, :].bitcast(FP8X4),
-                    scales=kk_s[:, h, :],
-                    in_=kk_bf[:, h, :, :].rearrange("p c t -> p (c t)"),
-                )
+            heads = slice(2 * pair, 2 * pair + 2)
+            nc.vector.quantize_mx(
+                out=kk_q[:, heads, :].rearrange("p h c -> p (h c)").bitcast(FP8X4),
+                scales=kk_s[:, heads, :].rearrange("p h c -> p (h c)"),
+                in_=kk_bf[:, heads, :, :].rearrange("p h c t -> p (h c t)"),
+            )
 
         def main_passes(g):
             if g % GROUPS == 0:
@@ -408,15 +407,15 @@ def tile_taylorsoftmaxattention_pa_t_kernel(
             v_masked = v_mask[g % 3][:].rearrange("p h x -> p (h x)")
             v_s = held["v_q", g][1]
             kk_q, kk_s = held["kk_q", g]
-            for h in HEAD_ORDER:
+            for h in range(H):
                 nc.tensor.matmul_mx(
                     out=z_main[:],
                     lhsT=v_masked[:, P * h : P * (h + 1)].bitcast(FP8X4),
-                    lhsT_scale=v_s[:],
+                    lhsT_scale=v_s,
                     rhs=kk_q[:, h, :].bitcast(FP8X4),
                     rhs_scale=kk_s[:, h, :],
-                    start=(g % GROUPS == 0 and h == HEAD_ORDER[0]),
-                    stop=(g % GROUPS == GROUPS - 1 and h == HEAD_ORDER[-1]),
+                    start=(g % GROUPS == 0 and h == 0),
+                    stop=(g % GROUPS == GROUPS - 1 and h == H - 1),
                 )
 
         def float_sums(g):
@@ -461,8 +460,8 @@ def tile_taylorsoftmaxattention_pa_t_kernel(
                 v_q, v_s = held["v_q", g]
                 nc.tensor.matmul_mx(
                     out=sums[:, 0, :],
-                    lhsT=v_q[:].bitcast(FP8X4),
-                    lhsT_scale=v_s[:],
+                    lhsT=v_q.bitcast(FP8X4),
+                    lhsT_scale=v_s,
                     rhs=tail_q[g % 3][:].bitcast(FP8X4),
                     rhs_scale=tail_s[g % 3][:],
                     start=(part == 0),
@@ -474,20 +473,19 @@ def tile_taylorsoftmaxattention_pa_t_kernel(
                 kn_q, kn_s = held["kn_q", g]
                 nc.tensor.matmul_mx(
                     out=sums[:, 1, :],
-                    lhsT=kn_q[:].bitcast(FP8X4),
-                    lhsT_scale=kn_s[:],
-                    rhs=v_q[:].bitcast(FP8X4),
-                    rhs_scale=v_s[:],
+                    lhsT=kn_q.bitcast(FP8X4),
+                    lhsT_scale=kn_s,
+                    rhs=v_q.bitcast(FP8X4),
+                    rhs_scale=v_s,
                     start=(part == 0),
                     stop=(part == GROUPS - 1),
                 )
             tail_sb = work.tile([P, TAIL // H], F32, tag="tail_sb")
             kv_tile = held["kv_tile", b]
-            copy = nc.vector.tensor_copy if b == B - 1 else nc.scalar.copy
             for h in range(H):
                 own = slice(D * h, D * (h + 1))
-                copy(out=tail_sb[own, :], in_=sums[own, 0, TAIL // H * h : TAIL // H * (h + 1)])
-                copy(out=kv_tile[own, 1 : D + 1], in_=sums[own, 1, own])
+                nc.scalar.copy(out=tail_sb[own, :], in_=sums[own, 0, TAIL // H * h : TAIL // H * (h + 1)])
+                nc.scalar.copy(out=kv_tile[own, 1 : D + 1], in_=sums[own, 1, own])
             nc.sync.dma_start(out=out_1[b].rearrange("h d c -> (h d) c"), in_=kv_tile[:])
             held["tail_sb", b] = tail_sb
 
@@ -622,41 +620,44 @@ def tile_taylorsoftmaxattention_pa_t_kernel(
                 v_to_tokens(g + 1)
             if done >= 0 and not last_of_batch:
                 tail_and_kv(done)
-            if done >= 0 and last_of_batch:
-                kv_mod_out(done)
             if g + 2 < n_groups:
                 sum_squares(g + 2)
-            float_sums(g)
+            if not following:
+                float_sums(g)
+                float_columns(g // GROUPS)
+            if done >= 0 and last_of_batch:
+                kv_mod_out(done)
+            if following:
+                float_sums(g)
             if last_of_batch:
                 main_passes(g - 1)
             if following:
                 norm(g + 1)
                 copy_kn(g + 1)
             strips(g)
-            quantise_v(g)
-            quantise_kn(g)
+            quantise_tail(g)
             if g + 2 < n_groups:
                 floor_norm(g + 2)
-            quantise_tail(g)
-            if not following:
-                mask_v(g)
-            quantise_products(g, HEAD_ORDER[:1])
-            if g + 2 < n_groups:
-                factors(g + 2)
             if g + 3 < n_groups:
                 quantise_x(g + 3)
-            quantise_products(g, HEAD_ORDER[1:])
+            if g + 2 < n_groups:
+                factors(g + 2)
+            quantise_v_kn(g)
+            if not following:
+                mask_v(g)
+            quantise_products(g, 0)
+            quantise_products(g, 1)
             if g == n_groups - 2:
                 vsum_out()
             if following:
                 first_products(g + 1)
-            if last_of_batch:
+            if last_of_batch and following:
                 float_columns(g // GROUPS)
             if done >= 0 and not last_of_batch:
                 spread_blocks(done)
                 spread_strips(done)
-        main_passes(n_groups - 1)
         tail_and_kv(B - 1)
+        main_passes(n_groups - 1)
         spread_blocks(B - 1)
         spread_strips(B - 1)
         kv_mod_out(B - 1)

@@ -31,6 +31,7 @@ TAIL_STRIP = 3
 STRIPS = (0, 1, 2, 4, 5, 6)
 STRIP_START = {0: 416, 1: 444, 2: 468, 4: 488, 5: 500, 6: 508}
 TAIL = H * N_BLK * (BLK - 1 - TAIL_STRIP)
+HEAD_ORDER = (2, 3, 0, 1)
 X_AHEAD = 6
 L_PITCH = N_BLK * (D + BLK)
 GPSIMD_HEADS = 3
@@ -48,7 +49,6 @@ def tile_taylorsoftmaxattention_pa_t_kernel(
         x_pool = ctx.enter_context(tc.tile_pool(name="x_pool", bufs=6))
         work = ctx.enter_context(tc.tile_pool(name="work", bufs=2))
         words = ctx.enter_context(tc.tile_pool(name="words", bufs=3))
-        single = ctx.enter_context(tc.tile_pool(name="single", bufs=1))
         turn_ps = ctx.enter_context(tc.psum_pool(name="turn_ps", bufs=4))
         ktok_ps = ctx.enter_context(tc.psum_pool(name="ktok_ps", bufs=2))
         main_ps = ctx.enter_context(tc.psum_pool(name="main_ps", bufs=1))
@@ -302,14 +302,11 @@ def tile_taylorsoftmaxattention_pa_t_kernel(
             move = nc.vector.tensor_copy if g == n_groups - 1 else nc.scalar.dma_start
             move(out=v_mask[g % 3][:, :, 0:D], in_=held["v_q", g][0].rearrange("p (h e) -> p h e", h=H))
 
-        def new_products(g):
-            kk_bf = single.tile([P, H, MAIN, PACK], BF16, tag="kk_bf", align_bytes=64)
-            kk_tail = single.tile([P, TAIL, PACK], BF16, tag="kk_tail", align_bytes=64)
-            held["kk_bf", g] = (kk_bf, kk_tail)
+        kk_bf = const.tile([P, H, MAIN, PACK], BF16, align_bytes=64)
+        kk_tail = const.tile([P, TAIL, PACK], BF16, align_bytes=64)
 
         def large_blocks(g):
             k_tok, k_r2, kn = held["k_tok", g], held["k_r2", g], held["kn", g]
-            kk_bf = held["kk_bf", g][0]
             shape = [P, GPSIMD_HEADS, HALF, HALF, PACK]
             kn_halves = kn[:].rearrange("p (b h i) t -> p b h i t", b=2, h=H)
             nc.gpsimd.tensor_tensor(
@@ -339,7 +336,7 @@ def tile_taylorsoftmaxattention_pa_t_kernel(
             k_tok, k_r2 = held["k_tok", g], held["k_r2", g]
             shape = [P, H, 2, BLK, BLK, PACK]
             nc.vector.tensor_tensor(
-                out=held["kk_bf", g][0][:, :, MID_START:DIAG_START, :].rearrange(
+                out=kk_bf[:, :, MID_START:DIAG_START, :].rearrange(
                     "p h (b a c) t -> p h b a c t", b=2, a=BLK
                 ),
                 in0=k_tok[:, :, 0 : P // 2]
@@ -354,7 +351,7 @@ def tile_taylorsoftmaxattention_pa_t_kernel(
             )
 
         def diagonal(g):
-            kk_bf, kn = held["kk_bf", g][0], held["kn", g]
+            kn = held["kn", g]
             nc.scalar.activation(
                 out=kk_bf[:, :, DIAG_START : DIAG_START + D, :].rearrange("p h (b x) t -> p h b x t", b=2),
                 in_=kn[:].rearrange("p (b h x) t -> p h b x t", b=2, h=H),
@@ -364,7 +361,6 @@ def tile_taylorsoftmaxattention_pa_t_kernel(
         def strips(g):
             k_rows = held["k_tok", g][:].rearrange("p t (s h b a) -> p s h b a t", s=2, h=H, b=2)
             k_cols = held["k_r2", g][:].rearrange("p (h b s a) t -> p s h b a t", s=2, h=H, b=2)
-            kk_bf, kk_tail = held["kk_bf", g]
             for a in range(BLK - 1):
                 width = BLK - 1 - a
                 if a == TAIL_STRIP:
@@ -382,7 +378,7 @@ def tile_taylorsoftmaxattention_pa_t_kernel(
             nc.vector.quantize_mx(
                 out=tail_q[g % 3][:, 0:TAIL].bitcast(FP8X4),
                 scales=tail_s[g % 3][:, 0:TAIL],
-                in_=held["kk_bf", g][1][:].rearrange("p c t -> p (c t)"),
+                in_=kk_tail[:].rearrange("p c t -> p (c t)"),
             )
 
         def quantise_products(g, pair):
@@ -390,7 +386,6 @@ def tile_taylorsoftmaxattention_pa_t_kernel(
                 kk_q = words.tile([P, H, MAIN], U32, tag="kk_q", align_bytes=64)
                 kk_s = words.tile([P, H, MAIN], U8, tag="kk_s", align_bytes=64)
                 held["kk_q", g] = (kk_q, kk_s)
-            kk_bf = held["kk_bf", g][0]
             kk_q, kk_s = held["kk_q", g]
             heads = slice(2 * pair, 2 * pair + 2)
             nc.vector.quantize_mx(
@@ -407,15 +402,15 @@ def tile_taylorsoftmaxattention_pa_t_kernel(
             v_masked = v_mask[g % 3][:].rearrange("p h x -> p (h x)")
             v_s = held["v_q", g][1]
             kk_q, kk_s = held["kk_q", g]
-            for h in range(H):
+            for h in HEAD_ORDER:
                 nc.tensor.matmul_mx(
                     out=z_main[:],
                     lhsT=v_masked[:, P * h : P * (h + 1)].bitcast(FP8X4),
                     lhsT_scale=v_s,
                     rhs=kk_q[:, h, :].bitcast(FP8X4),
                     rhs_scale=kk_s[:, h, :],
-                    start=(g % GROUPS == 0 and h == 0),
-                    stop=(g % GROUPS == GROUPS - 1 and h == H - 1),
+                    start=(g % GROUPS == 0 and h == HEAD_ORDER[0]),
+                    stop=(g % GROUPS == GROUPS - 1 and h == HEAD_ORDER[-1]),
                 )
 
         def float_sums(g):
@@ -563,9 +558,12 @@ def tile_taylorsoftmaxattention_pa_t_kernel(
                 out=out_2.rearrange("b h o c -> b (h o c)"), in_=vsum_tile[0:B].rearrange("p h c -> p (h c)")
             )
 
-        def first_products(g):
-            new_products(g)
+        def first_products(g, factor_of):
+            if factor_of < n_groups:
+                floor_norm(factor_of)
             large_blocks(g)
+            if factor_of < n_groups:
+                factors(factor_of)
             small_blocks(g)
 
         turn_x(0, (0, 2, 1, 3), (2, 3))
@@ -577,8 +575,8 @@ def tile_taylorsoftmaxattention_pa_t_kernel(
         nc.scalar.copy(out=bias_col[:, 0:1], in_=bias_ps[:, 0:1])
         nc.scalar.mul(out=bias_col[:, 1:2], in_=bias_ps[:, 1:2], mul=1.0 / N_TOK)
         quantise_x(0)
-        turn_x(1, (0, 1, 2, 3), (1, 3))
         project(0)
+        turn_x(1, (0, 1, 2, 3), (1, 3))
         quantise_x(1)
         sum_squares(0)
         k_to_tokens(0)
@@ -587,11 +585,12 @@ def tile_taylorsoftmaxattention_pa_t_kernel(
         root(0)
         norm(0)
         project(1)
-        first_products(0)
+        first_products(0, n_groups)
+        strips(0)
+        sum_squares(1)
+        turn_x(2, (0, 1, 2, 3))
         v_to_tokens(0)
         copy_kn(0)
-        turn_x(2, (0, 1, 2, 3))
-        sum_squares(1)
         floor_norm(1)
         factors(1)
         quantise_x(2)
@@ -601,13 +600,13 @@ def tile_taylorsoftmaxattention_pa_t_kernel(
             following = g + 1 < n_groups
             if g + X_AHEAD < n_groups:
                 load(g + X_AHEAD)
-            if following:
-                root(g + 1)
             if g >= 1:
                 mask_v(g - 1)
             if g + 3 < n_groups:
                 turn_x(g + 3, (0, 1))
             diagonal(g)
+            if following:
+                root(g + 1)
             if following:
                 k_to_tokens(g + 1)
             if g + 3 < n_groups:
@@ -634,23 +633,20 @@ def tile_taylorsoftmaxattention_pa_t_kernel(
             if following:
                 norm(g + 1)
                 copy_kn(g + 1)
-            strips(g)
+            if g > 0:
+                strips(g)
             quantise_tail(g)
-            if g + 2 < n_groups:
-                floor_norm(g + 2)
             if g + 3 < n_groups:
                 quantise_x(g + 3)
-            if g + 2 < n_groups:
-                factors(g + 2)
             quantise_v_kn(g)
             if not following:
                 mask_v(g)
-            quantise_products(g, 0)
             quantise_products(g, 1)
+            quantise_products(g, 0)
             if g == n_groups - 2:
                 vsum_out()
             if following:
-                first_products(g + 1)
+                first_products(g + 1, g + 2)
             if last_of_batch and following:
                 float_columns(g // GROUPS)
             if done >= 0 and not last_of_batch:

@@ -112,13 +112,13 @@ def tile_taylorsoftmaxattention_pa_t_kernel(
         nc.vector.tensor_reduce(
             out=rep_one[:], in_=ident[:].rearrange("k (h i) -> k i h", h=H), axis=AX.X, op=ALU.add
         )
-        rep = const.tile([P, N_BLK, D], F32)
-        nc.vector.tensor_copy(out=rep[:], in_=rep_one[:].unsqueeze(1).to_broadcast([P, N_BLK, D]))
-        rep_head = const.tile([P, H, P], F32)
-        nc.vector.memset(rep_head[:], 0.0)
-        for h in range(H):
-            own = slice(D * h, D * (h + 1))
-            nc.vector.tensor_copy(out=rep_head[own, h, :], in_=rep[own].rearrange("k J i -> k (J i)"))
+        spread_to = const.tile([P, N_BLK, P], F32)
+        nc.vector.memset(spread_to[:], 0.0)
+        for J in range(N_BLK):
+            nc.vector.tensor_copy(out=spread_to[:, J, D * J : D * (J + 1)], in_=rep_one[:])
+        mn_own = [const.tile([P, P], F32, name="mn_own%d" % n) for n in range(2)]
+        for n in range(2):
+            nc.gpsimd.memset(mn_own[n][:], 0.0)
         of_head = const.tile([P, H], F32)
         nc.vector.tensor_reduce(
             out=of_head[:], in_=ident[:].rearrange("k (s h x) -> k h s x", s=2, h=H), axis=AX.XY, op=ALU.add
@@ -433,20 +433,21 @@ def tile_taylorsoftmaxattention_pa_t_kernel(
             kv_tile = work.tile([P, D + 1], F32, tag="kv_tile")
             held["o_tile", b] = o_tile
             held["kv_tile", b] = kv_tile
-            mn = held["mn", b]
-            mn_sb = work.tile([P, P + 1], F32, tag="mn_sb")
-            nc.scalar.mul(out=mn_sb[:], in_=mn[:], mul=1.0 / N_TOK)
-            nc.scalar.copy(out=kv_tile[:, 0:1], in_=mn_sb[:, P : P + 1])
-            q = misc_ps.tile([P, P], F32, tag="misc")
+            mn, own_blocks = held["mn", b], mn_own[b % 2]
             for h in range(H):
                 own = slice(D * h, D * (h + 1))
-                nc.tensor.matmul(out=q[:, own], lhsT=rep_head[:, h, :], rhs=mn_sb[:, own], start=True, stop=True)
+                nc.scalar.mul(out=own_blocks[own, own], in_=mn[own, own], mul=1.0 / N_TOK)
+            nc.scalar.mul(out=kv_tile[:, 0:1], in_=mn[:, P : P + 1], mul=1.0 / N_TOK)
+            q = misc_ps.tile([P, D], F32, tag="misc")
             for J in range(N_BLK):
-                rows = slice(D * J, D * (J + 1))
-                nc.scalar.copy(
-                    out=o_tile[rows, :, :, 0:1],
-                    in_=q[rows, :].rearrange("p (h j) -> p h j", h=H)[:, :, BLK * J : BLK * (J + 1)].unsqueeze(3),
+                nc.tensor.matmul(
+                    out=q[:],
+                    lhsT=spread_to[:, J, :],
+                    rhs=own_blocks[:].rearrange("p (h j) -> p h j", h=H)[:, :, BLK * J : BLK * (J + 1)],
+                    start=(J == 0),
+                    stop=(J == N_BLK - 1),
                 )
+            nc.scalar.copy(out=o_tile[:, :, :, 0:1], in_=q[:].rearrange("p (h l) -> p h l", h=H).unsqueeze(3))
 
         def tail_and_kv(b):
             sums = turn_ps.tile([P, 2, P], F32, tag="turn", name="tail_and_kv_sums")

from contextlib import ExitStack

import concourse.mybir as mybir
from concourse.masks import make_identity

F32 = mybir.dt.float32
BF16 = mybir.dt.bfloat16
U8 = mybir.dt.uint8
U32 = mybir.dt.uint32
I32 = mybir.dt.int32
FP8X4 = mybir.dt.float8_e4m3fn_x4
ACT = mybir.ActivationFunctionType
ALU = mybir.AluOpType
AX = mybir.AxisListType

P = 128
PACK = 4
K_PASS = P * PACK
B, N_TOK, C, H, D = 8, 1024, 1024, 4, 32
GROUPS = N_TOK // K_PASS
C_PASSES = C // K_PASS
EPS = 1e-12
SCALE_SQ = 32.0**0.5
BLK = 8
N_BLK = D // BLK
HALF = D // 2
MAIN = 512
MID_START = HALF * HALF
DIAG_START = MID_START + 2 * BLK * BLK
TAIL_STRIP = 3
STRIPS = (0, 1, 2, 4, 5, 6)
STRIP_START = {0: 416, 1: 444, 2: 468, 4: 488, 5: 500, 6: 508}
TAIL = H * N_BLK * (BLK - 1 - TAIL_STRIP)
HEAD_ORDER = (2, 3, 0, 1)
X_AHEAD = 6
L_PITCH = N_BLK * (D + BLK)
GPSIMD_HEADS = 3
VECTOR_ROWS = ((3, 0), (3, BLK))

FLOPS = 2 * B * N_TOK * C * 2 * H * D + 2 * B * H * N_TOK * D * D * D + 2 * B * H * N_TOK * D * D


def tile_taylorsoftmaxattention_pa_t_kernel(
    tc, x, Wk_words, Wk_scales, bk, Wv_words, Wv_scales, bv, out_0, out_1, out_2
):
    nc = tc.nc
    with ExitStack() as ctx:
        const = ctx.enter_context(tc.tile_pool(name="const", bufs=1))
        x_pool = ctx.enter_context(tc.tile_pool(name="x_pool", bufs=6))
        work = ctx.enter_context(tc.tile_pool(name="work", bufs=2))
        words = ctx.enter_context(tc.tile_pool(name="words", bufs=3))
        turn_ps = ctx.enter_context(tc.psum_pool(name="turn_ps", bufs=4))
        ktok_ps = ctx.enter_context(tc.psum_pool(name="ktok_ps", bufs=2))
        main_ps = ctx.enter_context(tc.psum_pool(name="main_ps", bufs=1))
        misc_ps = ctx.enter_context(tc.psum_pool(name="misc_ps", bufs=1))
        ctx.enter_context(tc.manual_schedule())

        n_groups = B * GROUPS
        held = {}

        def load(g):
            b, part = divmod(g, GROUPS)
            xs = x_pool.tile([P, PACK, C], BF16, tag="xs")
            rows = x[b, K_PASS * part : K_PASS * (part + 1), :].rearrange("(p t) c -> p t c", t=PACK)
            pieces = 2 if g == 0 else 1
            for n in range(pieces):
                tokens = slice(PACK // pieces * n, PACK // pieces * (n + 1))
                nc.sync.dma_start(out=xs[:, tokens, :], in_=rows[:, tokens, :])
            held["xs", g] = xs

        load(0)

        ident = const.tile([P, P], F32)
        make_identity(nc, ident[:])

        w_words = const.tile([P, 2 * C_PASSES, P], U32, align_bytes=64)
        w_scales = const.tile([P, 2 * C_PASSES, P], U8, align_bytes=64)
        nc.vector.memset(w_scales[:].bitcast(I32), 0)
        for w, (codes, scales) in enumerate(((Wk_words, Wk_scales), (Wv_words, Wv_scales))):
            for c in range(C_PASSES):
                nc.sync.dma_start(
                    out=w_words[:, C_PASSES * w + c, :].bitcast(I32),
                    in_=codes[c].rearrange("p n t -> p (n t)").bitcast(I32),
                )
            for quad in range(4):
                nc.sync.dma_start(
                    out=w_scales[32 * quad : 32 * quad + 4, C_PASSES * w : C_PASSES * (w + 1), :].bitcast(I32),
                    in_=scales[:, 4 * quad : 4 * quad + 4, :].rearrange("c r n -> r c n").bitcast(I32),
                )

        k_words = const.tile([P, C_PASSES, P], I32, align_bytes=64)
        k_scales = const.tile([P, C_PASSES, P], U8, align_bytes=64)
        for to, given in ((k_words, w_words[:, 0:C_PASSES, :].bitcast(I32)), (k_scales, w_scales[:, 0:C_PASSES, :])):
            for half in range(2):
                nc.gpsimd.tensor_copy(
                    out=to[:, :, P // 2 * half : P // 2 * (half + 1)].rearrange("p c (m a) -> p c m a", a=BLK),
                    in_=given.rearrange("p c (m s a) -> p c m s a", s=2, a=BLK)[:, :, :, half, :],
                )

        bias_rows = const.tile([P, P], BF16)
        nc.vector.memset(bias_rows[:], 0.0)
        nc.sync.dma_start(
            out=bias_rows[0:1, :].rearrange("p (s m a) -> p s m a", s=2, a=BLK),
            in_=bk.rearrange("(m s a) -> s m a", s=2, a=BLK).unsqueeze(0),
        )
        nc.sync.dma_start(out=bias_rows[1:2, :], in_=bv.unsqueeze(0))
        load(1)
        load(2)
        for g in range(3, X_AHEAD):
            load(g)
        rep_one = const.tile([P, D], F32)
        nc.vector.tensor_reduce(
            out=rep_one[:], in_=ident[:].rearrange("k (h i) -> k i h", h=H), axis=AX.X, op=ALU.add
        )
        spread_to = const.tile([P, N_BLK, P], F32)
        nc.vector.memset(spread_to[:], 0.0)
        for J in range(N_BLK):
            nc.vector.tensor_copy(out=spread_to[:, J, D * J : D * (J + 1)], in_=rep_one[:])
        mn_own = [const.tile([P, P], F32, name="mn_own%d" % n) for n in range(2)]
        for n in range(2):
            nc.gpsimd.memset(mn_own[n][:], 0.0)
        of_head = const.tile([P, H], F32)
        nc.vector.tensor_reduce(
            out=of_head[:], in_=ident[:].rearrange("k (s h x) -> k h s x", s=2, h=H), axis=AX.XY, op=ALU.add
        )
        ones = const.tile([P, PACK], F32)
        nc.vector.memset(ones[:], 1.0)

        v_mask = [const.tile([P, H, P + D], I32, name="v_mask%d" % n, align_bytes=64) for n in range(3)]
        kn_tok = [const.tile([P, PACK, P + 4], F32, name="kn_tok%d" % n) for n in range(4)]
        for n in range(3):
            nc.gpsimd.memset(v_mask[n][:], 0)
        tail_q = [const.tile([P, P], I32, name="tail_q%d" % n, align_bytes=64) for n in range(3)]
        tail_s = [const.tile([P, P], U8, name="tail_s%d" % n, align_bytes=64) for n in range(3)]
        for n in range(3):
            nc.gpsimd.memset(tail_q[n][:], 0)
            nc.gpsimd.memset(tail_s[n][:].bitcast(I32), 0)
        for n in range(4):
            nc.scalar.copy(out=kn_tok[n][:, :, P : P + 1], in_=ones[:].unsqueeze(2))
        v_sums = const.tile([P, B * GROUPS], F32)
        sums_sq = const.tile([P, P], F32)
        nc.gpsimd.memset(sums_sq[:], 0.0)
        vsum_tile = const.tile([P, H, D + 1], F32)
        nc.gpsimd.memset(vsum_tile[0:D, :, 0:1], 1.0)

        def turn_x(g, quarters, by_vector=()):
            xs = held["xs", g]
            if 0 in quarters:
                x_grouped = work.tile([P, C_PASSES * K_PASS * PACK], BF16, tag="x_grouped", align_bytes=64)
                held["x_grouped", g] = x_grouped
            grouped_words = held["x_grouped", g][:].bitcast(F32).rearrange("p (c n u) -> p c n u", c=C_PASSES, u=2)
            for quarter in quarters:
                c, half = divmod(quarter, 2)
                turned = turn_ps.tile([P, 2, 2 * P], F32, tag="turn")
                for u in range(2):
                    for tl in range(2):
                        x_words = xs[:, 2 * half + tl, :].bitcast(F32)
                        nc.tensor.transpose(
                            turned[:, u, P * tl : P * (tl + 1)],
                            x_words[:, 256 * c + u : 256 * (c + 1) : 2],
                            ident[:],
                        )
                out = grouped_words[:, c, 2 * P * half : 2 * P * (half + 1), :]
                if quarter in by_vector:
                    nc.vector.tensor_copy(out=out, in_=turned[:].rearrange("p u n -> p n u"))
                else:
                    nc.scalar.copy(out=out, in_=turned[:].rearrange("p u n -> p n u"))

        def quantise_x(g):
            x_q = work.tile([P, C_PASSES * K_PASS], U32, tag="x_q", align_bytes=64)
            x_s = work.tile([P, C_PASSES * K_PASS], U8, tag="x_s", align_bytes=64)
            nc.vector.quantize_mx(out=x_q[:].bitcast(FP8X4), scales=x_s[:], in_=held["x_grouped", g][:])
            held["x_q", g] = (x_q, x_s)

        def project(g):
            x_q, x_s = held["x_q", g]
            sums = []
            given = (k_words[:].bitcast(U32), k_scales[:]), (w_words[:, C_PASSES:], w_scales[:, C_PASSES:])
            for words_of, scales_of in given:
                acc = turn_ps.tile([P, K_PASS], F32, tag="turn", name="acc")
                for c in range(C_PASSES):
                    cols = slice(K_PASS * c, K_PASS * (c + 1))
                    nc.tensor.matmul_mx(
                        out=acc[:],
                        lhsT=words_of[:, c, :].bitcast(FP8X4),
                        lhsT_scale=scales_of[:, c, :],
                        rhs=x_q[:, cols].bitcast(FP8X4),
                        rhs_scale=x_s[:, cols],
                        start=(c == 0),
                        stop=(c == C_PASSES - 1),
                    )
                sums.append(acc)
            kT = work.tile([P, K_PASS], F32, tag="kT")
            squares = work.tile([P, K_PASS], F32, tag="squares")
            vT = work.tile([P, K_PASS], F32, tag="vT")
            nc.scalar.activation(out=squares[:], in_=sums[0][:], func=ACT.Square, bias=bias_col[:, 0:1], scale=1.0)
            nc.scalar.activation(out=kT[:], in_=sums[0][:], func=ACT.Identity, bias=bias_col[:, 0:1], scale=1.0)
            nc.scalar.activation(
                out=vT[:],
                in_=sums[1][:],
                func=ACT.Identity,
                bias=bias_col[:, 1:2],
                scale=1.0 / N_TOK,
                accum_out=v_sums[:, g : g + 1],
            )
            held["kT", g] = kT
            held["squares", g] = squares
            held["vT", g] = vT

        def k_to_tokens(g):
            k_tok = ktok_ps.tile([P, PACK, P], F32, tag="k_tok")
            for t in range(PACK):
                nc.tensor.transpose(k_tok[:, t, :], held["kT", g][:, P * t : P * (t + 1)], ident[:])
            held["k_tok", g] = k_tok

        def sum_squares(g):
            sumsq = turn_ps.tile([P, PACK * H], F32, tag="turn", name="sumsq")
            for t in range(PACK):
                nc.tensor.matmul(
                    out=sumsq[:, H * t : H * (t + 1)],
                    lhsT=held["squares", g][:, P * t : P * (t + 1)],
                    rhs=of_head[:],
                    start=True,
                    stop=True,
                )
            held["sumsq", g] = sumsq

        def v_to_tokens(g):
            v_tok = turn_ps.tile([P, PACK, P], F32, tag="turn", name="v_tok")
            for t in range(PACK):
                nc.tensor.transpose(v_tok[:, t, :], held["vT", g][:, P * t : P * (t + 1)], ident[:])
            v_kn_bf = work.tile([P, 2, P, PACK], BF16, tag="v_kn_bf", align_bytes=64)
            nc.scalar.copy(out=v_kn_bf[:, 0], in_=v_tok[:].rearrange("p t f -> p f t"))
            held["v_kn_bf", g] = v_kn_bf

        def floor_norm(g):
            floored = work.tile([P, PACK * H], F32, tag="floored")
            nc.vector.tensor_scalar(
                out=floored[:],
                in0=held["sumsq", g][:],
                scalar1=EPS * EPS,
                scalar2=1.0 / SCALE_SQ,
                op0=ALU.max,
                op1=ALU.mult,
            )
            held["floored", g] = floored

        def factors(g):
            r2 = work.tile([P, PACK * H], F32, tag="r2")
            nc.vector.reciprocal(out=r2[:], in_=held["floored", g][:])
            held["r2", g] = r2

        def root(g):
            by_group = held["r2", g][:].unsqueeze(2).to_broadcast([P, PACK * H, 2])
            r1 = work.tile([P, PACK * H, 2], F32, tag="r1")
            nc.scalar.activation(out=r1[:], in_=by_group, func=ACT.Sqrt)
            r2 = work.tile([P, PACK * H, 2], F32, tag="r2_by_group")
            nc.scalar.copy(out=r2[:], in_=by_group)
            held["factors", g] = (r1, r2)

        def norm(g):
            for name, order, factor in zip(
                ("kn", "k_r2"), ("p (b h s a) t -> p s h b a t", "p (h b s a) t -> p s h b a t"), held["factors", g]
            ):
                scaled = work.tile([P, P, PACK], F32, tag=name, name=name)
                by_half = scaled[:].rearrange(order, h=H, b=2, s=2)
                for half in range(2):
                    nc.vector.tensor_tensor(
                        out=by_half[:, half],
                        in0=held["k_tok", g][:, :, P // 2 * half : P // 2 * (half + 1)].rearrange(
                            "p t (h b a) -> p h b a t", h=H, b=2
                        ),
                        in1=factor[:]
                        .rearrange("p (t h) b -> p h b t", h=H)
                        .unsqueeze(3)
                        .to_broadcast([P, H, 2, BLK, PACK]),
                        op=ALU.mult,
                    )
                held[name, g] = scaled

        def copy_kn(g):
            kn = held["kn", g][:].rearrange("p (b h x) t -> p b h x t", b=2, h=H)
            tok = kn_tok[g % 4][:, :, 0:P].rearrange("p t (h b x) -> p b h x t", b=2, h=H)
            for half in range(2):
                nc.scalar.copy(out=tok[:, half], in_=kn[:, half])
            nc.scalar.copy(
                out=held["v_kn_bf", g][:, 1].rearrange("p (h b x) t -> p b h x t", b=2, h=H), in_=kn
            )

        def quantise_v_kn(g):
            v_kn_q = words.tile([P, 2, P], I32, tag="v_kn_q", align_bytes=64)
            v_kn_s = words.tile([P, 2, P], U8, tag="v_kn_s", align_bytes=64)
            nc.vector.quantize_mx(
                out=v_kn_q[:].rearrange("p n f -> p (n f)").bitcast(FP8X4),
                scales=v_kn_s[:].rearrange("p n f -> p (n f)"),
                in_=held["v_kn_bf", g][:].rearrange("p n f t -> p (n f t)"),
            )
            held["v_q", g] = (v_kn_q[:, 0, :], v_kn_s[:, 0, :])
            held["kn_q", g] = (v_kn_q[:, 1, :], v_kn_s[:, 1, :])

        def mask_v(g):
            move = nc.vector.tensor_copy if g == n_groups - 1 else nc.scalar.dma_start
            move(out=v_mask[g % 3][:, :, 0:D], in_=held["v_q", g][0].rearrange("p (h e) -> p h e", h=H))

        kk_bf = const.tile([P, H, MAIN, PACK], BF16, align_bytes=64)
        kk_tail = const.tile([P, TAIL, PACK], BF16, align_bytes=64)

        def large_blocks(g):
            k_tok, k_r2, kn = held["k_tok", g], held["k_r2", g], held["kn", g]
            shape = [P, GPSIMD_HEADS, HALF, HALF, PACK]
            kn_halves = kn[:].rearrange("p (b h i) t -> p b h i t", b=2, h=H)
            nc.gpsimd.tensor_tensor(
                out=kk_bf[:, 0:GPSIMD_HEADS, 0:MID_START, :].rearrange("p h (i j) t -> p h i j t", i=HALF),
                in0=kn_halves[:, 0, 0:GPSIMD_HEADS].unsqueeze(3).to_broadcast(shape),
                in1=kn_halves[:, 1, 0:GPSIMD_HEADS].unsqueeze(2).to_broadcast(shape),
                op=ALU.mult,
            )
            for h, first_row in VECTOR_ROWS:
                half, a_first = divmod(first_row, BLK)
                rows = BLK - a_first
                i_first = P // 2 * half + 2 * BLK * h + a_first
                shape = [P, rows, HALF, PACK]
                nc.vector.tensor_tensor(
                    out=kk_bf[:, h, HALF * first_row : HALF * (first_row + rows), :].rearrange(
                        "p (i j) t -> p i j t", i=rows
                    ),
                    in0=k_tok[:, :, i_first : i_first + rows]
                    .rearrange("p t i -> p i t")
                    .unsqueeze(2)
                    .to_broadcast(shape),
                    in1=k_r2[:, D * h + HALF : D * (h + 1), :].unsqueeze(1).to_broadcast(shape),
                    op=ALU.mult,
                )

        def small_blocks(g):
            k_tok, k_r2 = held["k_tok", g], held["k_r2", g]
            shape = [P, H, 2, BLK, BLK, PACK]
            nc.vector.tensor_tensor(
                out=kk_bf[:, :, MID_START:DIAG_START, :].rearrange(
                    "p h (b a c) t -> p h b a c t", b=2, a=BLK
                ),
                in0=k_tok[:, :, 0 : P // 2]
                .rearrange("p t (h b a) -> p h b a t", h=H, b=2)
                .unsqueeze(4)
                .to_broadcast(shape),
                in1=k_r2[:]
                .rearrange("p (h b s c) t -> p s h b c t", h=H, b=2, s=2)[:, 1]
                .unsqueeze(3)
                .to_broadcast(shape),
                op=ALU.mult,
            )

        def diagonal(g):
            kn = held["kn", g]
            nc.scalar.activation(
                out=kk_bf[:, :, DIAG_START : DIAG_START + D, :].rearrange("p h (b x) t -> p h b x t", b=2),
                in_=kn[:].rearrange("p (b h x) t -> p h b x t", b=2, h=H),
                func=ACT.Square,
            )

        def strips(g):
            k_rows = held["k_tok", g][:].rearrange("p t (s h b a) -> p s h b a t", s=2, h=H, b=2)
            k_cols = held["k_r2", g][:].rearrange("p (h b s a) t -> p s h b a t", s=2, h=H, b=2)
            for a in range(BLK - 1):
                width = BLK - 1 - a
                if a == TAIL_STRIP:
                    out = kk_tail[:].rearrange("p (h x) t -> p h x t", h=H)
                else:
                    out = kk_bf[:, :, STRIP_START[a] : STRIP_START[a] + N_BLK * width, :]
                nc.vector.tensor_tensor(
                    out=out.rearrange("p h (s b w) t -> p s h b w t", s=2, b=2),
                    in0=k_rows[:, :, :, :, a : a + 1, :].to_broadcast([P, 2, H, 2, width, PACK]),
                    in1=k_cols[:, :, :, :, a + 1 : BLK, :],
                    op=ALU.mult,
                )

        def quantise_tail(g):
            nc.vector.quantize_mx(
                out=tail_q[g % 3][:, 0:TAIL].bitcast(FP8X4),
                scales=tail_s[g % 3][:, 0:TAIL],
                in_=kk_tail[:].rearrange("p c t -> p (c t)"),
            )

        def quantise_products(g, pair):
            if ("kk_q", g) not in held:
                kk_q = words.tile([P, H, MAIN], U32, tag="kk_q", align_bytes=64)
                kk_s = words.tile([P, H, MAIN], U8, tag="kk_s", align_bytes=64)
                held["kk_q", g] = (kk_q, kk_s)
            kk_q, kk_s = held["kk_q", g]
            heads = slice(2 * pair, 2 * pair + 2)
            nc.vector.quantize_mx(
                out=kk_q[:, heads, :].rearrange("p h c -> p (h c)").bitcast(FP8X4),
                scales=kk_s[:, heads, :].rearrange("p h c -> p (h c)"),
                in_=kk_bf[:, heads, :, :].rearrange("p h c t -> p (h c t)"),
            )

        def main_passes(g):
            if g % GROUPS == 0:
                z_main = main_ps.tile([P, MAIN], F32, tag="z_main")
                held["z_main", g // GROUPS] = z_main
            z_main = held["z_main", g // GROUPS]
            v_masked = v_mask[g % 3][:].rearrange("p h x -> p (h x)")
            v_s = held["v_q", g][1]
            kk_q, kk_s = held["kk_q", g]
            for h in HEAD_ORDER:
                nc.tensor.matmul_mx(
                    out=z_main[:],
                    lhsT=v_masked[:, P * h : P * (h + 1)].bitcast(FP8X4),
                    lhsT_scale=v_s,
                    rhs=kk_q[:, h, :].bitcast(FP8X4),
                    rhs_scale=kk_s[:, h, :],
                    start=(g % GROUPS == 0 and h == HEAD_ORDER[0]),
                    stop=(g % GROUPS == GROUPS - 1 and h == HEAD_ORDER[-1]),
                )

        def float_sums(g):
            b, part = divmod(g, GROUPS)
            if part == 0:
                mn = misc_ps.tile([P, P + 1], F32, tag="misc")
                held["mn", b] = mn
            mn, tok = held["mn", b], kn_tok[g % 4]
            for t in range(PACK):
                nc.tensor.matmul(
                    out=mn[:],
                    lhsT=tok[:, t, 0:P],
                    rhs=tok[:, t, 0 : P + 1],
                    start=(part == 0 and t == 0),
                    stop=(part == GROUPS - 1 and t == PACK - 1),
                )

        def float_columns(b):
            o_tile = work.tile([P, H, BLK, D + 1], F32, tag="o_tile")
            kv_tile = work.tile([P, D + 1], F32, tag="kv_tile")
            held["o_tile", b] = o_tile
            held["kv_tile", b] = kv_tile
            mn, own_blocks = held["mn", b], mn_own[b % 2]
            for h in range(H):
                own = slice(D * h, D * (h + 1))
                nc.scalar.mul(out=own_blocks[own, own], in_=mn[own, own], mul=1.0 / N_TOK)
            nc.scalar.mul(out=kv_tile[:, 0:1], in_=mn[:, P : P + 1], mul=1.0 / N_TOK)
            q = misc_ps.tile([P, D], F32, tag="misc")
            for J in range(N_BLK):
                nc.tensor.matmul(
                    out=q[:],
                    lhsT=spread_to[:, J, :],
                    rhs=own_blocks[:].rearrange("p (h j) -> p h j", h=H)[:, :, BLK * J : BLK * (J + 1)],
                    start=(J == 0),
                    stop=(J == N_BLK - 1),
                )
            nc.scalar.copy(out=o_tile[:, :, :, 0:1], in_=q[:].rearrange("p (h l) -> p h l", h=H).unsqueeze(3))

        def tail_and_kv(b):
            sums = turn_ps.tile([P, 2, P], F32, tag="turn", name="tail_and_kv_sums")
            for part in range(GROUPS):
                g = GROUPS * b + part
                v_q, v_s = held["v_q", g]
                nc.tensor.matmul_mx(
                    out=sums[:, 0, :],
                    lhsT=v_q.bitcast(FP8X4),
                    lhsT_scale=v_s,
                    rhs=tail_q[g % 3][:].bitcast(FP8X4),
                    rhs_scale=tail_s[g % 3][:],
                    start=(part == 0),
                    stop=(part == GROUPS - 1),
                )
            for part in range(GROUPS):
                g = GROUPS * b + part
                v_q, v_s = held["v_q", g]
                kn_q, kn_s = held["kn_q", g]
                nc.tensor.matmul_mx(
                    out=sums[:, 1, :],
                    lhsT=kn_q.bitcast(FP8X4),
                    lhsT_scale=kn_s,
                    rhs=v_q.bitcast(FP8X4),
                    rhs_scale=v_s,
                    start=(part == 0),
                    stop=(part == GROUPS - 1),
                )
            tail_sb = work.tile([P, TAIL // H], F32, tag="tail_sb")
            kv_tile = held["kv_tile", b]
            for h in range(H):
                own = slice(D * h, D * (h + 1))
                nc.scalar.copy(out=tail_sb[own, :], in_=sums[own, 0, TAIL // H * h : TAIL // H * (h + 1)])
                nc.scalar.copy(out=kv_tile[own, 1 : D + 1], in_=sums[own, 1, own])
            nc.sync.dma_start(out=out_1[b].rearrange("h d c -> (h d) c"), in_=kv_tile[:])
            held["tail_sb", b] = tail_sb

        def spread_blocks(b):
            z_main = held["z_main", b]
            z_sq = work.tile([P, BLK * L_PITCH + BLK], F32, tag="z_sq")
            rows = z_sq[:, 0 : BLK * L_PITCH].rearrange("p (l x) -> p l x", l=BLK)
            square = rows[:, :, 0:P].rearrange("p l (J i) -> p l J i", J=N_BLK)
            middle = rows.rearrange("p l (b x) -> p l b x", b=2)
            strip_results = z_main
            if b == B - 1:
                strip_results = work.tile([P, MAIN], F32, tag="strip_results")
                nc.vector.tensor_copy(out=strip_results[:, DIAG_START:MAIN], in_=z_main[:, DIAG_START:MAIN])
            held["strip_results", b] = strip_results
            z = z_main[:, 0:MID_START]
            nc.scalar.copy(out=square[:, :, 2:4, 0:HALF], in_=z.rearrange("p (i J l) -> p l J i", J=2, l=BLK))
            nc.scalar.copy(out=square[:, :, 0:2, HALF:D], in_=z.rearrange("p (J l j) -> p l J j", J=2, l=BLK))
            z = z_main[:, MID_START:DIAG_START]
            nc.scalar.copy(
                out=middle[:, :, :, D : D + BLK], in_=z.rearrange("p (b a l) -> p l b a", b=2, l=BLK)
            )
            nc.scalar.copy(
                out=middle[:, :, :, BLK : 2 * BLK], in_=z.rearrange("p (b l c) -> p l b c", b=2, l=BLK)
            )
            held["z_sq", b] = z_sq

        def spread_strips(b):
            z_sq, results, tail_sb = held["z_sq", b], held["strip_results", b], held["tail_sb", b]
            diagonal = z_sq[:, 0 : BLK * L_PITCH].rearrange("p (l G x) -> p l G x", l=BLK, G=N_BLK)
            copy = nc.vector.tensor_copy if b == B - 1 else nc.scalar.copy
            copy(
                out=z_sq[:].rearrange("p (a x) -> p a x", a=BLK)[:, :, 0:L_PITCH].rearrange(
                    "p a (G x) -> p a G x", G=N_BLK
                )[:, :, :, 0],
                in_=results[:, DIAG_START : DIAG_START + D].rearrange("p (G a) -> p a G", G=N_BLK),
            )
            for a in range(BLK - 1):
                width = BLK - 1 - a
                z = tail_sb[:] if a == TAIL_STRIP else results[:, STRIP_START[a] : STRIP_START[a] + N_BLK * width]
                z = z.rearrange("p (s b w) -> p s b w", s=2, b=2)
                copy(
                    out=diagonal[:, a + 1 : BLK, :, a].rearrange("p w (b s) -> p s b w", s=2), in_=z
                )
                copy(out=diagonal[:, a, :, a + 1 : BLK].rearrange("p (b s) w -> p s b w", s=2), in_=z)

        def kv_mod_out(b):
            o_tile, z_sq = held["o_tile", b], held["z_sq", b]
            for half in range(2):
                turned = turn_ps.tile([P, PACK, P], F32, tag="turn")
                for n in range(PACK):
                    nc.tensor.transpose(
                        turned[:, n, :], z_sq[:, L_PITCH * (PACK * half + n) : L_PITCH * (PACK * half + n) + P], ident[:]
                    )
                copy = nc.vector.tensor_copy if b == B - 1 and half == 1 else nc.scalar.copy
                copy(
                    out=o_tile[:, :, PACK * half : PACK * (half + 1), 1 : D + 1],
                    in_=turned[:].rearrange("p l (h e) -> p h l e", h=H),
                )
            for J in range(N_BLK):
                nc.sync.dma_start(
                    out=out_0[b, :, :, BLK * J : BLK * (J + 1), :].rearrange("h i l c -> i h (l c)"),
                    in_=o_tile[D * J : D * (J + 1)].rearrange("p h l c -> p h (l c)"),
                )

        def vsum_out():
            nc.vector.tensor_tensor(
                out=sums_sq[:, 0:B], in0=v_sums[:, 0 : B * GROUPS : 2], in1=v_sums[:, 1 : B * GROUPS : 2], op=ALU.add
            )
            sums_ps = turn_ps.tile([P, P], F32, tag="turn", name="sums_ps")
            nc.tensor.transpose(sums_ps[:], sums_sq[:], ident[:])
            nc.scalar.copy(
                out=vsum_tile[0:D, :, 1 : D + 1], in_=sums_ps[0:D, :].rearrange("p (h e) -> p h e", h=H)
            )
            nc.sync.dma_start(
                out=out_2.rearrange("b h o c -> b (h o c)"), in_=vsum_tile[0:B].rearrange("p h c -> p (h c)")
            )

        def first_products(g, factor_of):
            if factor_of < n_groups:
                floor_norm(factor_of)
            large_blocks(g)
            if factor_of < n_groups:
                factors(factor_of)
            small_blocks(g)

        turn_x(0, (0, 2, 1, 3), (2, 3))
        bias_rows_f = const.tile([P, P], F32)
        nc.vector.tensor_copy(out=bias_rows_f[:], in_=bias_rows[:])
        bias_ps = turn_ps.tile([P, P], F32, tag="turn")
        nc.tensor.transpose(bias_ps[:], bias_rows_f[:], ident[:])
        bias_col = const.tile([P, 2], F32)
        nc.scalar.copy(out=bias_col[:, 0:1], in_=bias_ps[:, 0:1])
        nc.scalar.mul(out=bias_col[:, 1:2], in_=bias_ps[:, 1:2], mul=1.0 / N_TOK)
        quantise_x(0)
        project(0)
        turn_x(1, (0, 1, 2, 3), (1, 3))
        quantise_x(1)
        sum_squares(0)
        k_to_tokens(0)
        floor_norm(0)
        factors(0)
        root(0)
        norm(0)
        project(1)
        first_products(0, n_groups)
        strips(0)
        sum_squares(1)
        turn_x(2, (0, 1, 2, 3))
        v_to_tokens(0)
        copy_kn(0)
        floor_norm(1)
        factors(1)
        quantise_x(2)
        for g in range(n_groups):
            last_of_batch = g % GROUPS == GROUPS - 1
            done = g // GROUPS - 1
            following = g + 1 < n_groups
            if g + X_AHEAD < n_groups:
                load(g + X_AHEAD)
            if g >= 1:
                mask_v(g - 1)
            if g + 3 < n_groups:
                turn_x(g + 3, (0, 1))
            diagonal(g)
            if following:
                root(g + 1)
            if following:
                k_to_tokens(g + 1)
            if g + 3 < n_groups:
                turn_x(g + 3, (2, 3))
            if g + 2 < n_groups:
                project(g + 2)
            if g >= 1 and not last_of_batch:
                main_passes(g - 1)
            if following:
                v_to_tokens(g + 1)
            if done >= 0 and not last_of_batch:
                tail_and_kv(done)
            if g + 2 < n_groups:
                sum_squares(g + 2)
            if not following:
                float_sums(g)
                float_columns(g // GROUPS)
            if done >= 0 and last_of_batch:
                kv_mod_out(done)
            if following:
                float_sums(g)
            if last_of_batch:
                main_passes(g - 1)
            if following:
                norm(g + 1)
                copy_kn(g + 1)
            if g > 0:
                strips(g)
            quantise_tail(g)
            if g + 3 < n_groups:
                quantise_x(g + 3)
            quantise_v_kn(g)
            if not following:
                mask_v(g)
            quantise_products(g, 1)
            quantise_products(g, 0)
            if g == n_groups - 2:
                vsum_out()
            if following:
                first_products(g + 1, g + 2)
            if last_of_batch and following:
                float_columns(g // GROUPS)
            if done >= 0 and not last_of_batch:
                spread_blocks(done)
                spread_strips(done)
        tail_and_kv(B - 1)
        main_passes(n_groups - 1)
        spread_blocks(B - 1)
        spread_strips(B - 1)
        kv_mod_out(B - 1)
